import numpy as np
import ml_dtypes


def mxq(x, axis, fmt="e4m3"):
    dtype, down = {"e4m3": (ml_dtypes.float8_e4m3fn, 7), "e5m2": (ml_dtypes.float8_e5m2, 14)}[fmt]
    v = np.moveaxis(np.asarray(x, np.float32).astype(ml_dtypes.bfloat16).astype(np.float64), axis, -1)
    blocks = v.reshape(v.shape[:-1] + (-1, 32))
    amax = np.abs(blocks).max(-1, keepdims=True)
    byte = np.maximum(np.where(amax > 0, np.frexp(amax)[1] - 1 + 127, 0) - down, 1)
    scale = np.exp2(byte - 127.0)
    codes = (blocks / scale).astype(np.float32).astype(dtype).astype(np.float64)
    return np.moveaxis((codes * scale).reshape(v.shape), -1, axis)


WIDE = False


def mx_kscale(k):
    if not WIDE:
        return np.ones(k)
    levels = np.array([10, -10, 5, -5, 0])
    a = np.random.permutation(np.resize(levels, k // 512 * 4)).reshape(k // 512, 4)
    idx = np.arange(k)
    return np.exp2(a[idx // 512, idx % 128 // 32])


BF16 = ml_dtypes.bfloat16


def bf(x):
    return np.asarray(x, np.float32).astype(BF16)


def f64(x):
    return np.asarray(x).astype(np.float64)


B, T, D, H, E, C = 2, 1024, 1024, 8, 1024, 512
HD = D // H
QC = 4.0


def setup_inputs():
    theta = np.exp(0.2 * np.random.standard_normal(H)) / 10000.0 ** (2.0 * np.arange(H) / H)
    f = np.array(mx_kscale(T), dtype=np.float64)
    f[:HD] = f.min()
    a = 1.0 / np.exp(-theta * 0.25 * T).mean()
    q = np.random.standard_normal((B, T, H, HD))
    k = np.random.standard_normal((B, T, H, HD))
    v = np.random.standard_normal((B, T, H, HD))
    q[..., 0] = QC
    k[..., 0] -= a * np.log(f)[None, :, None] * np.sqrt(HD) / QC
    v *= (f / f.min())[None, :, None, None]
    return {"q": bf(q), "k": bf(k), "v": bf(v), "theta": bf(theta)}


def reference(q, k, v, theta):
    qh = f64(q).transpose(0, 2, 1, 3)
    kt = f64(k).transpose(0, 2, 3, 1)
    vq = mxq(f64(v).transpose(0, 2, 1, 3), 2, "e4m3")
    th = f64(theta)
    pos = np.arange(T, dtype=np.float64)
    blocks = []
    for r in range(0, T, C):
        n = pos[r:r + C, None] - pos[None, :r + C]
        decay = np.where(n >= 0, np.exp(-th[None, None, :] * np.maximum(n, 0.0)[:, :, None]).mean(-1), 0.0)
        s = qh[:, :, r:r + C] @ kt[:, :, :, :r + C] / np.sqrt(HD)
        s = np.where(n >= 0, s * decay, -np.inf)
        e = np.exp(s - s.max(-1, keepdims=True))
        blocks.append((mxq(e, 3, "e4m3") @ vq[:, :, :r + C]) / e.sum(-1, keepdims=True))
    return np.concatenate(blocks, 2).transpose(0, 2, 1, 3)

@@ -1,0 +1,325 @@
+from contextlib import ExitStack
+import math
+
+import concourse.mybir as mybir
+from concourse.masks import make_identity
+
+F32 = mybir.dt.float32
+BF16 = mybir.dt.bfloat16
+I32 = mybir.dt.int32
+U32 = mybir.dt.uint32
+U8 = mybir.dt.uint8
+FP8X4 = mybir.dt.float8_e4m3fn_x4
+ALU = mybir.AluOpType
+FUNC = mybir.ActivationFunctionType
+AXIS = mybir.AxisListType
+
+B, T, H, HD = 2, 1024, 8, 128
+P = 128
+PACK = 4
+K_PASS = P * PACK
+BANK = 512
+NT = T // P
+HEADS = B * H
+FLOPS = 4 * B * H * HD * (K_PASS * K_PASS + K_PASS * T)
+
+TABLE_SCALE = -1.0 / (H * math.sqrt(HD))
+SHUT_OUT = -(2.0 ** 100)
+
+LAG_EXP = 1
+LAG_TRANSPOSE = 2
+LAG_QUANTISE = 3
+LAG_MULTIPLY = 4
+LAG_STORE = 5
+TRANSPOSE_Q_AFTER = 2
+TRANSPOSE_K_AFTER = 5
+
+
+def passes_of(i):
+    return (i * P) // K_PASS + 1
+
+
+def tile_retentivenetwork_pa_kernel(tc, q, k, v, theta, out):
+    nc = tc.nc
+    with ExitStack() as ctx:
+        const = ctx.enter_context(tc.tile_pool(name="const", bufs=1))
+        table_pool = ctx.enter_context(tc.tile_pool(name="table", bufs=3))
+        value_pool = ctx.enter_context(tc.tile_pool(name="values", bufs=2))
+        raw_pool = ctx.enter_context(tc.tile_pool(name="raw", bufs=3))
+        cols_pool = ctx.enter_context(tc.tile_pool(name="cols", bufs=2))
+        stat_pool = ctx.enter_context(tc.tile_pool(name="stats", bufs=3))
+        work = ctx.enter_context(tc.tile_pool(name="work", bufs=3))
+        ps_scores = ctx.enter_context(tc.psum_pool(name="ps_scores", bufs=3))
+        ps_words = ctx.enter_context(tc.psum_pool(name="ps_words", bufs=2))
+        ps_out = ctx.enter_context(tc.psum_pool(name="ps_out", bufs=2))
+        ps_rows = ctx.enter_context(tc.psum_pool(name="ps_rows", bufs=1))
+
+        theta_bf = const.tile([P, H], BF16)
+        nc.sync.dma_start(out=theta_bf[:], in_=theta.partition_broadcast(P))
+
+        distance = const.tile([P, T], F32)
+        nc.gpsimd.iota(
+            distance[:],
+            pattern=[[-1, T]],
+            base=T - P,
+            channel_multiplier=1,
+            allow_small_or_imprecise_dtypes=True,
+        )
+        ident_bf = const.tile([P, P], BF16)
+        make_identity(nc, ident_bf[:])
+        ident_f32 = const.tile([P, P], F32)
+        make_identity(nc, ident_f32[:])
+
+        shut_out = const.tile([P, P], BF16)
+        nc.vector.tensor_scalar(
+            out=shut_out[:],
+            in0=distance[:, T - P : T],
+            scalar1=0.0,
+            scalar2=SHUT_OUT,
+            op0=ALU.is_lt,
+            op1=ALU.mult,
+        )
+        nc.vector.tensor_scalar_max(
+            out=distance[:, T - P : T], in0=distance[:, T - P : T], scalar1=0.0
+        )
+        neg_theta = const.tile([P, H], F32)
+        nc.vector.tensor_scalar_mul(out=neg_theta[:], in0=theta_bf[:], scalar1=-1.0)
+
+        e_tiles = {}
+        for i in range(NT):
+            for parity in range(2):
+                e_tile = const.tile(
+                    [P, 2, passes_of(i) * P, 2], BF16, name="e_%d_%d" % (i, parity)
+                )
+                e_tiles[(i, parity)] = e_tile
+                if (i + 1) * P < passes_of(i) * K_PASS:
+                    nc.vector.memset(
+                        e_tile[:].rearrange("q u a e -> q (u a e)").bitcast(I32), 0
+                    )
+
+        v_codes = const.tile([P, B * 2, H * HD], U32, align_bytes=64)
+        v_scales = const.tile([P, B * 2, H * HD], U8, align_bytes=64)
+        v_raw = {}
+
+        def load_values(b):
+            for g in range(T // K_PASS):
+                raw = value_pool.tile([P, PACK, H * HD], BF16, name="v_raw")
+                nc.sync.dma_start(
+                    out=raw[:],
+                    in_=v[b, g * K_PASS : (g + 1) * K_PASS].rearrange(
+                        "(p t) h d -> p t (h d)", t=PACK
+                    ),
+                )
+                v_raw[(b, g)] = raw
+
+        def quantise_values(b):
+            for g in range(T // K_PASS):
+                grouped = value_pool.tile([P, H * HD, PACK], BF16, name="v_grouped", align_bytes=64)
+                nc.vector.tensor_copy(
+                    out=grouped[:].rearrange("p (c r) t -> p c t r", r=4),
+                    in_=v_raw[(b, g)][:].rearrange("p t (c r) -> p c t r", r=4),
+                )
+                nc.vector.quantize_mx(
+                    out=v_codes[:, b * 2 + g, :].bitcast(FP8X4),
+                    scales=v_scales[:, b * 2 + g, :],
+                    in_=grouped[:].rearrange("p w t -> p (w t)"),
+                )
+
+        heads = {}
+
+        def load_head(hd):
+            b, h = divmod(hd, H)
+            q_raw = raw_pool.tile([P, NT, HD], BF16, name="q_raw")
+            nc.sync.dma_start(out=q_raw[:], in_=q[b, :, h, :].rearrange("(n p) d -> p n d", p=P))
+            k_raw = raw_pool.tile([P, NT, HD], BF16, name="k_raw")
+            nc.sync.dma_start(out=k_raw[:], in_=k[b, :, h, :].rearrange("(n p) d -> p n d", p=P))
+            heads[hd] = {"q_raw": q_raw, "k_raw": k_raw}
+
+        def transpose_rows(hd, which):
+            rows_ps = ps_rows.tile([P, NT, P], BF16, name="rows_ps")
+            for n in range(NT):
+                nc.tensor.transpose(rows_ps[:, n, :], heads[hd][which + "_raw"][:, n, :], ident_bf[:])
+            cols = cols_pool.tile([P, T], BF16, name=which + "_cols")
+            nc.scalar.copy(out=cols[:], in_=rows_ps[:].rearrange("d n p -> d (n p)"))
+            heads[hd][which] = cols
+
+        load_head(0)
+        load_values(0)
+        load_head(1)
+
+        neg_weight = const.tile([P, T], F32)
+        for half in (1, 0):
+            cols = slice(half * BANK, (half + 1) * BANK)
+            for c in range(H):
+                decay = table_pool.tile([P, BANK], F32, name="decay")
+                nc.scalar.activation(
+                    out=decay[:], in_=distance[:, cols], func=FUNC.Exp, scale=neg_theta[:, c : c + 1]
+                )
+                if c == 0:
+                    nc.vector.tensor_scalar_mul(out=neg_weight[:, cols], in0=decay[:], scalar1=TABLE_SCALE)
+                else:
+                    nc.vector.scalar_tensor_tensor(
+                        out=neg_weight[:, cols],
+                        in0=decay[:],
+                        scalar=TABLE_SCALE,
+                        in1=neg_weight[:, cols],
+                        op0=ALU.mult,
+                        op1=ALU.add,
+                    )
+
+        transpose_rows(0, "q")
+        transpose_rows(0, "k")
+        quantise_values(0)
+
+        units = [(hd, i) for hd in range(HEADS) for i in range(NT)]
+        live = {}
+
+        def scores(u):
+            hd, i = units[u]
+            if i == 0:
+                heads[hd]["neg_max"] = stat_pool.tile([P, NT], F32, name="neg_max")
+                heads[hd]["row_sum"] = stat_pool.tile([P, NT], F32, name="row_sum")
+                if hd + 2 < HEADS:
+                    load_head(hd + 2)
+                if (hd + 2) % H == 0 and hd + 2 < HEADS:
+                    load_values((hd + 2) // H)
+                if (hd + 1) % H == 0 and hd + 1 < HEADS:
+                    quantise_values((hd + 1) // H)
+            keys = (i + 1) * P
+            banks = []
+            for k0 in range(0, keys, BANK):
+                width = min(BANK, keys - k0)
+                diagonal = k0 + width == keys
+                bank = ps_scores.tile([P, BANK], F32, name="scores_ps")
+                nc.tensor.matmul(
+                    out=bank[:, :width],
+                    lhsT=heads[hd]["q"][:, i * P : (i + 1) * P],
+                    rhs=heads[hd]["k"][:, k0 : k0 + width],
+                    start=True,
+                    stop=not diagonal,
+                )
+                if diagonal:
+                    nc.tensor.matmul(
+                        out=bank[:, width - P : width],
+                        lhsT=ident_bf[:],
+                        rhs=shut_out[:],
+                        start=False,
+                        stop=True,
+                    )
+                banks.append((k0, width, bank))
+            live[u] = {"banks": banks}
+            if hd + 1 < HEADS and i == TRANSPOSE_Q_AFTER:
+                transpose_rows(hd + 1, "q")
+            if hd + 1 < HEADS and i == TRANSPOSE_K_AFTER:
+                transpose_rows(hd + 1, "k")
+
+        def weigh(u):
+            hd, i = units[u]
+            keys = (i + 1) * P
+            neg_s = work.tile([P, T], F32, name="neg_s")
+            for k0, width, bank in live[u]["banks"]:
+                nc.vector.tensor_tensor(
+                    out=neg_s[:, k0 : k0 + width],
+                    in0=bank[:, :width],
+                    in1=neg_weight[:, T - keys + k0 : T - keys + k0 + width],
+                    op=ALU.mult,
+                )
+            nc.vector.tensor_reduce(
+                out=heads[hd]["neg_max"][:, i : i + 1], in_=neg_s[:, :keys], axis=AXIS.X, op=ALU.min
+            )
+            live[u]["neg_s"] = neg_s
+
+        def exponentials(u):
+            hd, i = units[u]
+            keys = (i + 1) * P
+            nc.scalar.activation(
+                out=e_tiles[(i, hd % 2)][:, :, 0 : keys // PACK, :],
+                in_=live[u]["neg_s"][:, :keys].rearrange("q (a u e) -> q u a e", u=2, e=2),
+                func=FUNC.Exp,
+                bias=heads[hd]["neg_max"][:, i : i + 1],
+                scale=-1.0,
+                accum_out=heads[hd]["row_sum"][:, i : i + 1],
+            )
+
+        def transposes(u):
+            hd, i = units[u]
+            passes = passes_of(i)
+            e_words = e_tiles[(i, hd % 2)][:].rearrange("q u a e -> q (u a e)").bitcast(F32)
+            words_ps = ps_words.tile([P, passes, 2, P], F32, name="words_ps")
+            for g in range(passes):
+                for half in range(2):
+                    first = half * passes * P + g * P
+                    nc.tensor.transpose(words_ps[:, g, half, :], e_words[:, first : first + P], ident_f32[:])
+            live[u]["words_ps"] = words_ps
+
+        def regroup(u):
+            hd, i = units[u]
+            passes = passes_of(i)
+            grouped = work.tile([P, passes * K_PASS], BF16, name="e_grouped", align_bytes=64)
+            nc.scalar.copy(
+                out=grouped[:].bitcast(F32).rearrange("p (g q u) -> p g q u", g=passes, u=2),
+                in_=live[u]["words_ps"][:].rearrange("p g u q -> p g q u"),
+            )
+            live[u]["grouped"] = grouped
+
+        def quantise(u):
+            hd, i = units[u]
+            passes = passes_of(i)
+            codes = work.tile([P, passes * P], U32, name="e_codes", align_bytes=64)
+            scales = work.tile([P, passes * P], U8, name="e_scales", align_bytes=64)
+            nc.vector.quantize_mx(out=codes[:].bitcast(FP8X4), scales=scales[:], in_=live[u]["grouped"][:])
+            live[u]["codes"] = codes
+            live[u]["scales"] = scales
+
+        def multiply_values(u):
+            hd, i = units[u]
+            b, h = divmod(hd, H)
+            if i % 4 == 0:
+                heads[hd]["acc"] = ps_out.tile([P, 4, HD], F32, name="acc")
+            passes = passes_of(i)
+            for g in range(passes):
+                nc.tensor.matmul_mx(
+                    out=heads[hd]["acc"][:, i % 4, :],
+                    lhsT=live[u]["codes"][:, g * P : (g + 1) * P].bitcast(FP8X4),
+                    lhsT_scale=live[u]["scales"][:, g * P : (g + 1) * P],
+                    rhs=v_codes[:, b * 2 + g, h * HD : (h + 1) * HD].bitcast(FP8X4),
+                    rhs_scale=v_scales[:, b * 2 + g, h * HD : (h + 1) * HD],
+                    start=(g == 0),
+                    stop=(g == passes - 1),
+                )
+            live[u]["acc"] = heads[hd]["acc"]
+
+        def store(u):
+            hd, i = units[u]
+            b, h = divmod(hd, H)
+            if i % 4 != 3:
+                return
+            inverse = stat_pool.tile([P, 4], F32, name="inverse")
+            nc.vector.reciprocal(out=inverse[:], in_=heads[hd]["row_sum"][:, i - 3 : i + 1])
+            result = work.tile([P, 4, HD], F32, name="result")
+            for s in range(4):
+                nc.scalar.activation(
+                    out=result[:, s, :],
+                    in_=live[u]["acc"][:, s, :],
+                    func=FUNC.Copy,
+                    scale=inverse[:, s : s + 1],
+                )
+            nc.scalar.dma_start(
+                out=out[b, (i - 3) * P : (i + 1) * P, h, :].rearrange("(s p) d -> p s d", p=P),
+                in_=result[:],
+            )
+
+        def run(stage, u):
+            if 0 <= u < len(units):
+                stage(u)
+
+        scores(0)
+        for step in range(len(units) + LAG_STORE):
+            run(transposes, step - LAG_TRANSPOSE)
+            run(multiply_values, step - LAG_MULTIPLY)
+            run(scores, step + 1)
+            run(exponentials, step - LAG_EXP)
+            run(regroup, step - LAG_TRANSPOSE)
+            run(store, step - LAG_STORE)
+            run(quantise, step - LAG_QUANTISE)
+            run(weigh, step)

@@ -27,10 +27,11 @@ TABLE_SCALE = -1.0 / (H * math.sqrt(HD))
 SHUT_OUT = -(2.0 ** 100)
 
 LAG_EXP = 1
-LAG_TRANSPOSE = 2
-LAG_QUANTISE = 3
-LAG_MULTIPLY = 4
-LAG_STORE = 5
+LAG_TRANSPOSE = 3
+LAG_REGROUP = 4
+LAG_QUANTISE = 5
+LAG_MULTIPLY = 6
+LAG_STORE = 7
 TRANSPOSE_Q_AFTER = 2
 TRANSPOSE_K_AFTER = 5
 
@@ -49,6 +50,7 @@ def tile_retentivenetwork_pa_kernel(tc, q, k, v, theta, out):
         cols_pool = ctx.enter_context(tc.tile_pool(name="cols", bufs=2))
         stat_pool = ctx.enter_context(tc.tile_pool(name="stats", bufs=3))
         work = ctx.enter_context(tc.tile_pool(name="work", bufs=3))
+        score_pool = ctx.enter_context(tc.tile_pool(name="neg_s", bufs=5))
         ps_scores = ctx.enter_context(tc.psum_pool(name="ps_scores", bufs=3))
         ps_words = ctx.enter_context(tc.psum_pool(name="ps_words", bufs=2))
         ps_out = ctx.enter_context(tc.psum_pool(name="ps_out", bufs=2))
@@ -93,9 +95,8 @@ def tile_retentivenetwork_pa_kernel(tc, q, k, v, theta, out):
                 )
                 e_tiles[(i, parity)] = e_tile
                 if (i + 1) * P < passes_of(i) * K_PASS:
-                    nc.vector.memset(
-                        e_tile[:].rearrange("q u a e -> q (u a e)").bitcast(I32), 0
-                    )
+                    e_pairs = e_tile[:].rearrange("q u a e -> q u (a e)").bitcast(I32)
+                    nc.vector.memset(e_pairs[:, :, (i + 1) * P // PACK :], 0)
 
         v_codes = const.tile([P, B * 2, H * HD], U32, align_bytes=64)
         v_scales = const.tile([P, B * 2, H * HD], U8, align_bytes=64)
@@ -112,17 +113,27 @@ def tile_retentivenetwork_pa_kernel(tc, q, k, v, theta, out):
                 )
                 v_raw[(b, g)] = raw
 
-        def quantise_values(b):
+        v_grouped = {}
+
+        def regroup_values(b):
             for g in range(T // K_PASS):
                 grouped = value_pool.tile([P, H * HD, PACK], BF16, name="v_grouped", align_bytes=64)
-                nc.vector.tensor_copy(
-                    out=grouped[:].rearrange("p (c r) t -> p c t r", r=4),
-                    in_=v_raw[(b, g)][:].rearrange("p t (c r) -> p c t r", r=4),
+                nc.gpsimd.tensor_scalar(
+                    out=grouped[:],
+                    in0=v_raw[(b, g)][:].rearrange("p t w -> p w t"),
+                    scalar1=1.0,
+                    scalar2=0.0,
+                    op0=ALU.mult,
+                    op1=ALU.add,
                 )
+                v_grouped[(b, g)] = grouped
+
+        def quantise_values(b):
+            for g in range(T // K_PASS):
                 nc.vector.quantize_mx(
                     out=v_codes[:, b * 2 + g, :].bitcast(FP8X4),
                     scales=v_scales[:, b * 2 + g, :],
-                    in_=grouped[:].rearrange("p w t -> p (w t)"),
+                    in_=v_grouped[(b, g)][:].rearrange("p w t -> p (w t)"),
                 )
 
         heads = {}
@@ -139,13 +150,17 @@ def tile_retentivenetwork_pa_kernel(tc, q, k, v, theta, out):
             rows_ps = ps_rows.tile([P, NT, P], BF16, name="rows_ps")
             for n in range(NT):
                 nc.tensor.transpose(rows_ps[:, n, :], heads[hd][which + "_raw"][:, n, :], ident_bf[:])
-            cols = cols_pool.tile([P, T], BF16, name=which + "_cols")
-            nc.scalar.copy(out=cols[:], in_=rows_ps[:].rearrange("d n p -> d (n p)"))
-            heads[hd][which] = cols
+            heads[hd][which + "_ps"] = rows_ps
+
+        def collect_rows(hd, which):
+            channels = cols_pool.tile([P, T], BF16, name=which + "_channels")
+            nc.scalar.copy(out=channels[:], in_=heads[hd][which + "_ps"][:].rearrange("d n p -> d (n p)"))
+            heads[hd][which] = channels
 
         load_head(0)
         load_values(0)
         load_head(1)
+        regroup_values(0)
 
         neg_weight = const.tile([P, T], F32)
         for half in (1, 0):
@@ -167,9 +182,9 @@ def tile_retentivenetwork_pa_kernel(tc, q, k, v, theta, out):
                         op1=ALU.add,
                     )
 
-        transpose_rows(0, "q")
-        transpose_rows(0, "k")
-        quantise_values(0)
+        for which in ("q", "k"):
+            transpose_rows(0, which)
+            collect_rows(0, which)
 
         units = [(hd, i) for hd in range(HEADS) for i in range(NT)]
         live = {}
@@ -184,7 +199,7 @@ def tile_retentivenetwork_pa_kernel(tc, q, k, v, theta, out):
                 if (hd + 2) % H == 0 and hd + 2 < HEADS:
                     load_values((hd + 2) // H)
                 if (hd + 1) % H == 0 and hd + 1 < HEADS:
-                    quantise_values((hd + 1) // H)
+                    regroup_values((hd + 1) // H)
             keys = (i + 1) * P
             banks = []
             for k0 in range(0, keys, BANK):
@@ -213,10 +228,17 @@ def tile_retentivenetwork_pa_kernel(tc, q, k, v, theta, out):
             if hd + 1 < HEADS and i == TRANSPOSE_K_AFTER:
                 transpose_rows(hd + 1, "k")
 
+        def next_head_rows(u):
+            hd, i = units[u]
+            if hd + 1 < HEADS and i == TRANSPOSE_Q_AFTER:
+                collect_rows(hd + 1, "q")
+            if hd + 1 < HEADS and i == TRANSPOSE_K_AFTER:
+                collect_rows(hd + 1, "k")
+
         def weigh(u):
             hd, i = units[u]
             keys = (i + 1) * P
-            neg_s = work.tile([P, T], F32, name="neg_s")
+            neg_s = score_pool.tile([P, T], F32, name="neg_s")
             for k0, width, bank in live[u]["banks"]:
                 nc.vector.tensor_tensor(
                     out=neg_s[:, k0 : k0 + width],
@@ -224,10 +246,16 @@ def tile_retentivenetwork_pa_kernel(tc, q, k, v, theta, out):
                     in1=neg_weight[:, T - keys + k0 : T - keys + k0 + width],
                     op=ALU.mult,
                 )
-            nc.vector.tensor_reduce(
-                out=heads[hd]["neg_max"][:, i : i + 1], in_=neg_s[:, :keys], axis=AXIS.X, op=ALU.min
-            )
             live[u]["neg_s"] = neg_s
+
+        def row_maximum(u):
+            hd, i = units[u]
+            nc.vector.tensor_reduce(
+                out=heads[hd]["neg_max"][:, i : i + 1],
+                in_=live[u]["neg_s"][:, : (i + 1) * P],
+                axis=AXIS.X,
+                op=ALU.min,
+            )
 
         def exponentials(u):
             hd, i = units[u]
@@ -264,6 +292,8 @@ def tile_retentivenetwork_pa_kernel(tc, q, k, v, theta, out):
 
         def quantise(u):
             hd, i = units[u]
+            if hd % H == 0 and i == 0:
+                quantise_values(hd // H)
             passes = passes_of(i)
             codes = work.tile([P, passes * P], U32, name="e_codes", align_bytes=64)
             scales = work.tile([P, passes * P], U8, name="e_scales", align_bytes=64)
@@ -319,7 +349,9 @@ def tile_retentivenetwork_pa_kernel(tc, q, k, v, theta, out):
             run(multiply_values, step - LAG_MULTIPLY)
             run(scores, step + 1)
             run(exponentials, step - LAG_EXP)
-            run(regroup, step - LAG_TRANSPOSE)
+            run(regroup, step - LAG_REGROUP)
+            run(next_head_rows, step)
             run(store, step - LAG_STORE)
-            run(quantise, step - LAG_QUANTISE)
             run(weigh, step)
+            run(quantise, step - LAG_QUANTISE)
+            run(row_maximum, step)

@@ -118,13 +118,9 @@ def tile_retentivenetwork_pa_kernel(tc, q, k, v, theta, out):
         def regroup_values(b):
             for g in range(T // K_PASS):
                 grouped = value_pool.tile([P, H * HD, PACK], BF16, name="v_grouped", align_bytes=64)
-                nc.gpsimd.tensor_scalar(
-                    out=grouped[:],
-                    in0=v_raw[(b, g)][:].rearrange("p t w -> p w t"),
-                    scalar1=1.0,
-                    scalar2=0.0,
-                    op0=ALU.mult,
-                    op1=ALU.add,
+                nc.vector.tensor_copy(
+                    out=grouped[:].rearrange("p (c r) t -> p c t r", r=4),
+                    in_=v_raw[(b, g)][:].rearrange("p t (c r) -> p c t r", r=4),
                 )
                 v_grouped[(b, g)] = grouped
 

@@ -59,33 +59,49 @@ def tile_retentivenetwork_pa_kernel(tc, q, k, v, theta, out):
         theta_bf = const.tile([P, H], BF16)
         nc.sync.dma_start(out=theta_bf[:], in_=theta.partition_broadcast(P))
 
-        distance = const.tile([P, T], F32)
+        distance = const.tile([P, P], F32)
         nc.gpsimd.iota(
             distance[:],
-            pattern=[[-1, T]],
-            base=T - P,
+            pattern=[[-1, P]],
+            base=0,
             channel_multiplier=1,
             allow_small_or_imprecise_dtypes=True,
         )
-        ident_bf = const.tile([P, P], BF16)
-        make_identity(nc, ident_bf[:])
         ident_f32 = const.tile([P, P], F32)
         make_identity(nc, ident_f32[:])
+        ident_bf = const.tile([P, P], BF16)
+        make_identity(nc, ident_bf[:])
+        upward = const.tile([P, P], F32)
+        nc.gpsimd.iota(
+            upward[:], pattern=[[1, P]], base=0, channel_multiplier=0, allow_small_or_imprecise_dtypes=True
+        )
+        backward = const.tile([P, T - P], F32)
+        nc.gpsimd.iota(
+            backward[:],
+            pattern=[[-1, T - P]],
+            base=T - P,
+            channel_multiplier=0,
+            allow_small_or_imprecise_dtypes=True,
+        )
 
         shut_out = const.tile([P, P], BF16)
         nc.vector.tensor_scalar(
             out=shut_out[:],
-            in0=distance[:, T - P : T],
+            in0=distance[:],
             scalar1=0.0,
             scalar2=SHUT_OUT,
             op0=ALU.is_lt,
             op1=ALU.mult,
         )
-        nc.vector.tensor_scalar_max(
-            out=distance[:, T - P : T], in0=distance[:, T - P : T], scalar1=0.0
-        )
+        nc.vector.tensor_scalar_max(out=distance[:], in0=distance[:], scalar1=0.0)
         neg_theta = const.tile([P, H], F32)
         nc.vector.tensor_scalar_mul(out=neg_theta[:], in0=theta_bf[:], scalar1=-1.0)
+        on_diagonal = const.tile([P, H], F32)
+        nc.vector.tensor_tensor(out=on_diagonal[:], in0=neg_theta[:], in1=ident_f32[:, 0:H], op=ALU.mult)
+        neg_rate = const.tile([P, 1], F32)
+        nc.vector.tensor_reduce(out=neg_rate[:], in_=on_diagonal[:], axis=AXIS.X, op=ALU.add)
+        is_rate = const.tile([P, 1], F32)
+        nc.vector.tensor_reduce(out=is_rate[:], in_=ident_f32[:, 0:H], axis=AXIS.X, op=ALU.add)
 
         e_tiles = {}
         for i in range(NT):
@@ -159,24 +175,45 @@ def tile_retentivenetwork_pa_kernel(tc, q, k, v, theta, out):
         regroup_values(0)
 
         neg_weight = const.tile([P, T], F32)
-        for half in (1, 0):
-            cols = slice(half * BANK, (half + 1) * BANK)
-            for c in range(H):
-                decay = table_pool.tile([P, BANK], F32, name="decay")
-                nc.scalar.activation(
-                    out=decay[:], in_=distance[:, cols], func=FUNC.Exp, scale=neg_theta[:, c : c + 1]
+        cols = slice(T - P, T)
+        for c in range(H):
+            decay = table_pool.tile([P, P], F32, name="decay")
+            nc.scalar.activation(
+                out=decay[:], in_=distance[:], func=FUNC.Exp, scale=neg_theta[:, c : c + 1]
+            )
+            if c == 0:
+                nc.vector.tensor_scalar_mul(out=neg_weight[:, cols], in0=decay[:], scalar1=TABLE_SCALE)
+            else:
+                nc.vector.scalar_tensor_tensor(
+                    out=neg_weight[:, cols],
+                    in0=decay[:],
+                    scalar=TABLE_SCALE,
+                    in1=neg_weight[:, cols],
+                    op0=ALU.mult,
+                    op1=ALU.add,
                 )
-                if c == 0:
-                    nc.vector.tensor_scalar_mul(out=neg_weight[:, cols], in0=decay[:], scalar1=TABLE_SCALE)
-                else:
-                    nc.vector.scalar_tensor_tensor(
-                        out=neg_weight[:, cols],
-                        in0=decay[:],
-                        scalar=TABLE_SCALE,
-                        in1=neg_weight[:, cols],
-                        op0=ALU.mult,
-                        op1=ALU.add,
-                    )
+        by_query = const.tile([P, P], F32)
+        nc.scalar.activation(out=by_query[:], in_=upward[:], func=FUNC.Exp, scale=neg_rate[:, 0:1])
+        by_query_scaled = const.tile([P, P], F32)
+        nc.vector.tensor_scalar(
+            out=by_query_scaled[:],
+            in0=by_query[:],
+            scalar1=is_rate[:, 0:1],
+            scalar2=TABLE_SCALE,
+            op0=ALU.mult,
+            op1=ALU.mult,
+        )
+        by_key = const.tile([P, T - P], F32)
+        for cols in (slice(BANK, T - P), slice(0, BANK)):
+            width = cols.stop - cols.start
+            nc.scalar.activation(
+                out=by_key[:, cols], in_=backward[:, cols], func=FUNC.Exp, scale=neg_rate[:, 0:1]
+            )
+            table_ps = ps_scores.tile([P, BANK], F32, name="scores_ps")
+            nc.tensor.matmul(
+                out=table_ps[:, :width], lhsT=by_query_scaled[:], rhs=by_key[:, cols], start=True, stop=True
+            )
+            nc.vector.tensor_copy(out=neg_weight[:, cols], in_=table_ps[:, :width])
 
         for which in ("q", "k"):
             transpose_rows(0, which)

@@ -114,13 +114,13 @@ def tile_retentivenetwork_pa_kernel(tc, q, k, v, theta, out):
                     e_pairs = e_tile[:].rearrange("q u a e -> q u (a e)").bitcast(I32)
                     nc.vector.memset(e_pairs[:, :, (i + 1) * P // PACK :], 0)
 
-        v_codes = const.tile([P, B * 2, H * HD], U32, align_bytes=64)
-        v_scales = const.tile([P, B * 2, H * HD], U8, align_bytes=64)
+        v_codes = const.tile([P, HEADS, T // K_PASS, HD], U32, align_bytes=64)
+        v_scales = const.tile([P, HEADS, T // K_PASS, HD], U8, align_bytes=64)
         v_raw = {}
 
         def load_values(b):
             for g in range(T // K_PASS):
-                raw = value_pool.tile([P, PACK, H * HD], BF16, name="v_raw")
+                raw = const.tile([P, PACK, H * HD], BF16, name="v_raw_%d_%d" % (b, g))
                 nc.sync.dma_start(
                     out=raw[:],
                     in_=v[b, g * K_PASS : (g + 1) * K_PASS].rearrange(
@@ -131,22 +131,26 @@ def tile_retentivenetwork_pa_kernel(tc, q, k, v, theta, out):
 
         v_grouped = {}
 
-        def regroup_values(b):
+        def regroup_values(hd):
+            b, h = divmod(hd, H)
+            grouped = value_pool.tile([P, T // K_PASS, HD, PACK], BF16, name="v_grouped", align_bytes=64)
             for g in range(T // K_PASS):
-                grouped = value_pool.tile([P, H * HD, PACK], BF16, name="v_grouped", align_bytes=64)
-                nc.vector.tensor_copy(
-                    out=grouped[:].rearrange("p (c r) t -> p c t r", r=4),
-                    in_=v_raw[(b, g)][:].rearrange("p t (c r) -> p c t r", r=4),
+                nc.gpsimd.tensor_scalar(
+                    out=grouped[:, g].rearrange("p (c r) t -> p c t r", r=4),
+                    in0=v_raw[(b, g)][:, :, h * HD : (h + 1) * HD].rearrange("p t (c r) -> p c t r", r=4),
+                    scalar1=1.0,
+                    scalar2=0.0,
+                    op0=ALU.mult,
+                    op1=ALU.add,
                 )
-                v_grouped[(b, g)] = grouped
+            v_grouped[hd] = grouped
 
-        def quantise_values(b):
-            for g in range(T // K_PASS):
-                nc.vector.quantize_mx(
-                    out=v_codes[:, b * 2 + g, :].bitcast(FP8X4),
-                    scales=v_scales[:, b * 2 + g, :],
-                    in_=v_grouped[(b, g)][:].rearrange("p w t -> p (w t)"),
-                )
+        def quantise_values(hd):
+            nc.vector.quantize_mx(
+                out=v_codes[:, hd].rearrange("p g c -> p (g c)").bitcast(FP8X4),
+                scales=v_scales[:, hd].rearrange("p g c -> p (g c)"),
+                in_=v_grouped[hd][:].rearrange("p g w t -> p (g w t)"),
+            )
 
         heads = {}
 
@@ -229,10 +233,10 @@ def tile_retentivenetwork_pa_kernel(tc, q, k, v, theta, out):
                 heads[hd]["row_sum"] = stat_pool.tile([P, NT], F32, name="row_sum")
                 if hd + 2 < HEADS:
                     load_head(hd + 2)
-                if (hd + 2) % H == 0 and hd + 2 < HEADS:
-                    load_values((hd + 2) // H)
-                if (hd + 1) % H == 0 and hd + 1 < HEADS:
-                    regroup_values((hd + 1) // H)
+                if hd == 4:
+                    load_values(1)
+            if i == 1 and hd + 1 < HEADS:
+                regroup_values(hd + 1)
             keys = (i + 1) * P
             banks = []
             for k0 in range(0, keys, BANK):
@@ -325,8 +329,10 @@ def tile_retentivenetwork_pa_kernel(tc, q, k, v, theta, out):
 
         def quantise(u):
             hd, i = units[u]
-            if hd % H == 0 and i == 0:
-                quantise_values(hd // H)
+            if u == 0:
+                quantise_values(0)
+            if i == 4 and hd + 1 < HEADS:
+                quantise_values(hd + 1)
             passes = passes_of(i)
             codes = work.tile([P, passes * P], U32, name="e_codes", align_bytes=64)
             scales = work.tile([P, passes * P], U8, name="e_scales", align_bytes=64)
@@ -345,8 +351,8 @@ def tile_retentivenetwork_pa_kernel(tc, q, k, v, theta, out):
                     out=heads[hd]["acc"][:, i % 4, :],
                     lhsT=live[u]["codes"][:, g * P : (g + 1) * P].bitcast(FP8X4),
                     lhsT_scale=live[u]["scales"][:, g * P : (g + 1) * P],
-                    rhs=v_codes[:, b * 2 + g, h * HD : (h + 1) * HD].bitcast(FP8X4),
-                    rhs_scale=v_scales[:, b * 2 + g, h * HD : (h + 1) * HD],
+                    rhs=v_codes[:, hd, g, :].bitcast(FP8X4),
+                    rhs_scale=v_scales[:, hd, g, :],
                     start=(g == 0),
                     stop=(g == passes - 1),
                 )

@@ -135,13 +135,9 @@ def tile_retentivenetwork_pa_kernel(tc, q, k, v, theta, out):
             b, h = divmod(hd, H)
             grouped = value_pool.tile([P, T // K_PASS, HD, PACK], BF16, name="v_grouped", align_bytes=64)
             for g in range(T // K_PASS):
-                nc.gpsimd.tensor_scalar(
+                nc.vector.tensor_copy(
                     out=grouped[:, g].rearrange("p (c r) t -> p c t r", r=4),
-                    in0=v_raw[(b, g)][:, :, h * HD : (h + 1) * HD].rearrange("p t (c r) -> p c t r", r=4),
-                    scalar1=1.0,
-                    scalar2=0.0,
-                    op0=ALU.mult,
-                    op1=ALU.add,
+                    in_=v_raw[(b, g)][:, :, h * HD : (h + 1) * HD].rearrange("p t (c r) -> p c t r", r=4),
                 )
             v_grouped[hd] = grouped
 
@@ -373,7 +369,7 @@ def tile_retentivenetwork_pa_kernel(tc, q, k, v, theta, out):
                     func=FUNC.Copy,
                     scale=inverse[:, s : s + 1],
                 )
-            nc.scalar.dma_start(
+            nc.sync.dma_start(
                 out=out[b, (i - 3) * P : (i + 1) * P, h, :].rearrange("(s p) d -> p s d", p=P),
                 in_=result[:],
             )

@@ -51,10 +51,9 @@ def tile_retentivenetwork_pa_kernel(tc, q, k, v, theta, out):
         stat_pool = ctx.enter_context(tc.tile_pool(name="stats", bufs=3))
         work = ctx.enter_context(tc.tile_pool(name="work", bufs=3))
         score_pool = ctx.enter_context(tc.tile_pool(name="neg_s", bufs=5))
-        ps_scores = ctx.enter_context(tc.psum_pool(name="ps_scores", bufs=3))
+        ps_scores = ctx.enter_context(tc.psum_pool(name="ps_scores", bufs=4))
         ps_words = ctx.enter_context(tc.psum_pool(name="ps_words", bufs=2))
         ps_out = ctx.enter_context(tc.psum_pool(name="ps_out", bufs=2))
-        ps_rows = ctx.enter_context(tc.psum_pool(name="ps_rows", bufs=1))
 
         theta_bf = const.tile([P, H], BF16)
         nc.sync.dma_start(out=theta_bf[:], in_=theta.partition_broadcast(P))
@@ -135,7 +134,8 @@ def tile_retentivenetwork_pa_kernel(tc, q, k, v, theta, out):
             b, h = divmod(hd, H)
             grouped = value_pool.tile([P, T // K_PASS, HD, PACK], BF16, name="v_grouped", align_bytes=64)
             for g in range(T // K_PASS):
-                nc.vector.tensor_copy(
+                copy = nc.vector.tensor_copy if g == 0 else nc.scalar.copy
+                copy(
                     out=grouped[:, g].rearrange("p (c r) t -> p c t r", r=4),
                     in_=v_raw[(b, g)][:, :, h * HD : (h + 1) * HD].rearrange("p t (c r) -> p c t r", r=4),
                 )
@@ -159,14 +159,14 @@ def tile_retentivenetwork_pa_kernel(tc, q, k, v, theta, out):
             heads[hd] = {"q_raw": q_raw, "k_raw": k_raw}
 
         def transpose_rows(hd, which):
-            rows_ps = ps_rows.tile([P, NT, P], BF16, name="rows_ps")
+            rows_ps = ps_words.tile([P, NT, P], BF16, name="words_ps")
             for n in range(NT):
                 nc.tensor.transpose(rows_ps[:, n, :], heads[hd][which + "_raw"][:, n, :], ident_bf[:])
             heads[hd][which + "_ps"] = rows_ps
 
-        def collect_rows(hd, which):
+        def collect_rows(hd, which, copy=nc.scalar.copy):
             channels = cols_pool.tile([P, T], BF16, name=which + "_channels")
-            nc.scalar.copy(out=channels[:], in_=heads[hd][which + "_ps"][:].rearrange("d n p -> d (n p)"))
+            copy(out=channels[:], in_=heads[hd][which + "_ps"][:].rearrange("d n p -> d (n p)"))
             heads[hd][which] = channels
 
         load_head(0)
@@ -175,6 +175,23 @@ def tile_retentivenetwork_pa_kernel(tc, q, k, v, theta, out):
         regroup_values(0)
 
         neg_weight = const.tile([P, T], F32)
+        by_query = const.tile([P, P], F32)
+        nc.scalar.activation(out=by_query[:], in_=upward[:], func=FUNC.Exp, scale=neg_rate[:, 0:1])
+        by_query_scaled = const.tile([P, P], F32)
+        nc.vector.tensor_scalar(
+            out=by_query_scaled[:],
+            in0=by_query[:],
+            scalar1=is_rate[:, 0:1],
+            scalar2=TABLE_SCALE,
+            op0=ALU.mult,
+            op1=ALU.mult,
+        )
+        by_key = const.tile([P, T - P], F32)
+        near, far = slice(BANK, T - P), slice(0, BANK)
+        nc.scalar.activation(
+            out=by_key[:, near], in_=backward[:, near], func=FUNC.Exp, scale=neg_rate[:, 0:1]
+        )
+
         cols = slice(T - P, T)
         for c in range(H):
             decay = table_pool.tile([P, P], F32, name="decay")
@@ -192,39 +209,31 @@ def tile_retentivenetwork_pa_kernel(tc, q, k, v, theta, out):
                     op0=ALU.mult,
                     op1=ALU.add,
                 )
-        by_query = const.tile([P, P], F32)
-        nc.scalar.activation(out=by_query[:], in_=upward[:], func=FUNC.Exp, scale=neg_rate[:, 0:1])
-        by_query_scaled = const.tile([P, P], F32)
-        nc.vector.tensor_scalar(
-            out=by_query_scaled[:],
-            in0=by_query[:],
-            scalar1=is_rate[:, 0:1],
-            scalar2=TABLE_SCALE,
-            op0=ALU.mult,
-            op1=ALU.mult,
-        )
-        by_key = const.tile([P, T - P], F32)
-        for cols in (slice(BANK, T - P), slice(0, BANK)):
+
+        transpose_rows(0, "q")
+        transpose_rows(0, "k")
+        collect_rows(0, "q")
+        collect_rows(0, "k", nc.vector.tensor_copy)
+
+        for cols in (near, far):
             width = cols.stop - cols.start
-            nc.scalar.activation(
-                out=by_key[:, cols], in_=backward[:, cols], func=FUNC.Exp, scale=neg_rate[:, 0:1]
-            )
+            if cols == far:
+                nc.scalar.activation(
+                    out=by_key[:, far], in_=backward[:, far], func=FUNC.Exp, scale=neg_rate[:, 0:1]
+                )
             table_ps = ps_scores.tile([P, BANK], F32, name="scores_ps")
             nc.tensor.matmul(
                 out=table_ps[:, :width], lhsT=by_query_scaled[:], rhs=by_key[:, cols], start=True, stop=True
             )
             nc.vector.tensor_copy(out=neg_weight[:, cols], in_=table_ps[:, :width])
 
-        for which in ("q", "k"):
-            transpose_rows(0, which)
-            collect_rows(0, which)
-
-        units = [(hd, i) for hd in range(HEADS) for i in range(NT)]
+        units = [(hd, i) for hd in range(HEADS - 1) for i in range(NT)]
+        units.extend([(HEADS - 1, i) for i in reversed(range(NT))])
         live = {}
 
         def scores(u):
             hd, i = units[u]
-            if i == 0:
+            if u % NT == 0:
                 heads[hd]["neg_max"] = stat_pool.tile([P, NT], F32, name="neg_max")
                 heads[hd]["row_sum"] = stat_pool.tile([P, NT], F32, name="row_sum")
                 if hd + 2 < HEADS:
@@ -339,7 +348,7 @@ def tile_retentivenetwork_pa_kernel(tc, q, k, v, theta, out):
         def multiply_values(u):
             hd, i = units[u]
             b, h = divmod(hd, H)
-            if i % 4 == 0:
+            if u % 4 == 0:
                 heads[hd]["acc"] = ps_out.tile([P, 4, HD], F32, name="acc")
             passes = passes_of(i)
             for g in range(passes):
@@ -357,10 +366,11 @@ def tile_retentivenetwork_pa_kernel(tc, q, k, v, theta, out):
         def store(u):
             hd, i = units[u]
             b, h = divmod(hd, H)
-            if i % 4 != 3:
+            if u % 4 != 3:
                 return
+            first = i - i % 4
             inverse = stat_pool.tile([P, 4], F32, name="inverse")
-            nc.vector.reciprocal(out=inverse[:], in_=heads[hd]["row_sum"][:, i - 3 : i + 1])
+            nc.vector.reciprocal(out=inverse[:], in_=heads[hd]["row_sum"][:, first : first + 4])
             result = work.tile([P, 4, HD], F32, name="result")
             for s in range(4):
                 nc.scalar.activation(
@@ -370,7 +380,7 @@ def tile_retentivenetwork_pa_kernel(tc, q, k, v, theta, out):
                     scale=inverse[:, s : s + 1],
                 )
             nc.sync.dma_start(
-                out=out[b, (i - 3) * P : (i + 1) * P, h, :].rearrange("(s p) d -> p s d", p=P),
+                out=out[b, first * P : (first + 4) * P, h, :].rearrange("(s p) d -> p s d", p=P),
                 in_=result[:],
             )
 

@@ -93,6 +93,8 @@ def tile_retentivenetwork_pa_kernel(tc, q, k, v, theta, out):
             op1=ALU.mult,
         )
         nc.vector.tensor_scalar_max(out=distance[:], in0=distance[:], scalar1=0.0)
+        minus_one = const.tile([P, 4], F32)
+        nc.gpsimd.memset(minus_one[:], -1.0)
         neg_theta = const.tile([P, H], F32)
         nc.vector.tensor_scalar_mul(out=neg_theta[:], in0=theta_bf[:], scalar1=-1.0)
         on_diagonal = const.tile([P, H], F32)
@@ -110,8 +112,8 @@ def tile_retentivenetwork_pa_kernel(tc, q, k, v, theta, out):
                 )
                 e_tiles[(i, parity)] = e_tile
                 if (i + 1) * P < passes_of(i) * K_PASS:
-                    e_pairs = e_tile[:].rearrange("q u a e -> q u (a e)").bitcast(I32)
-                    nc.vector.memset(e_pairs[:, :, (i + 1) * P // PACK :], 0)
+                    e_pairs = e_tile[:].rearrange("q u a e -> q u (a e)").bitcast(F32)
+                    nc.gpsimd.memset(e_pairs[:, :, (i + 1) * P // PACK :], 0.0)
 
         v_codes = const.tile([P, HEADS, T // K_PASS, HD], U32, align_bytes=64)
         v_scales = const.tile([P, HEADS, T // K_PASS, HD], U8, align_bytes=64)
@@ -370,7 +372,9 @@ def tile_retentivenetwork_pa_kernel(tc, q, k, v, theta, out):
                 return
             first = i - i % 4
             inverse = stat_pool.tile([P, 4], F32, name="inverse")
-            nc.vector.reciprocal(out=inverse[:], in_=heads[hd]["row_sum"][:, first : first + 4])
+            nc.gpsimd.tensor_tensor(
+                out=inverse[:], in0=heads[hd]["row_sum"][:, first : first + 4], in1=minus_one[:], op=ALU.pow
+            )
             result = work.tile([P, 4, HD], F32, name="result")
             for s in range(4):
                 nc.scalar.activation(

@@ -168,7 +168,10 @@ def tile_retentivenetwork_pa_kernel(tc, q, k, v, theta, out):
 
         def collect_rows(hd, which, copy=nc.scalar.copy):
             channels = cols_pool.tile([P, T], BF16, name=which + "_channels")
-            copy(out=channels[:], in_=heads[hd][which + "_ps"][:].rearrange("d n p -> d (n p)"))
+            copy(
+                out=channels[:].bitcast(F32),
+                in_=heads[hd][which + "_ps"][:].rearrange("d n p -> d (n p)").bitcast(F32),
+            )
             heads[hd][which] = channels
 
         load_head(0)

@@ -36,8 +36,23 @@ TRANSPOSE_Q_AFTER = 2
 TRANSPOSE_K_AFTER = 5
 
 
+ORDER = (7, 0, 6, 1, 5, 2, 4, 3)
+RIDERS = (0, 1, 2)
+HOSTS = (4, 5, 6)
+QUADRANT = 32
+BANK_TILES = ((0, 1, 6, 7), (2, 3, 4, 5))
+BANK_FULL_AFTER = (5, 3)
+CODE_WORDS = HD
+BLOCK_WORDS = HD + HD // 4
+
+
 def passes_of(i):
     return (i * P) // K_PASS + 1
+
+
+def column_of(i):
+    bank = 0 if i in BANK_TILES[0] else 1
+    return bank, BANK_TILES[bank].index(i)
 
 
 def tile_retentivenetwork_pa_kernel(tc, q, k, v, theta, out):
@@ -106,17 +121,19 @@ def tile_retentivenetwork_pa_kernel(tc, q, k, v, theta, out):
 
         e_tiles = {}
         for i in range(NT):
+            if i in RIDERS:
+                continue
             for parity in range(2):
-                e_tile = const.tile(
+                e_tiles[(i, parity)] = const.tile(
                     [P, 2, passes_of(i) * P, 2], BF16, name="e_%d_%d" % (i, parity)
                 )
-                e_tiles[(i, parity)] = e_tile
-                if (i + 1) * P < passes_of(i) * K_PASS:
-                    e_pairs = e_tile[:].rearrange("q u a e -> q u (a e)").bitcast(F32)
-                    nc.gpsimd.memset(e_pairs[:, :, (i + 1) * P // PACK :], 0.0)
 
-        v_codes = const.tile([P, HEADS, T // K_PASS, HD], U32, align_bytes=64)
-        v_scales = const.tile([P, HEADS, T // K_PASS, HD], U8, align_bytes=64)
+        v_blocks = const.tile([P, HEADS, T // K_PASS, BLOCK_WORDS], U32, align_bytes=64)
+        nc.vector.memset(
+            v_blocks[:].rearrange("p h g w -> p (h g) w")[:, :, CODE_WORDS:].bitcast(I32), 0
+        )
+        v_shared = const.tile([P, 2, len(HOSTS), 2, BLOCK_WORDS], U32, align_bytes=64)
+        nc.vector.memset(v_shared[:].rearrange("p s j b w -> p (s j b w)").bitcast(I32), 0)
         v_raw = {}
 
         def load_values(b):
@@ -144,11 +161,22 @@ def tile_retentivenetwork_pa_kernel(tc, q, k, v, theta, out):
             v_grouped[hd] = grouped
 
         def quantise_values(hd):
-            nc.vector.quantize_mx(
-                out=v_codes[:, hd].rearrange("p g c -> p (g c)").bitcast(FP8X4),
-                scales=v_scales[:, hd].rearrange("p g c -> p (g c)"),
-                in_=v_grouped[hd][:].rearrange("p g w t -> p (g w t)"),
-            )
+            for g in range(T // K_PASS):
+                nc.vector.quantize_mx(
+                    out=v_blocks[:, hd, g, :CODE_WORDS].bitcast(FP8X4),
+                    scales=v_blocks[:, hd, g, CODE_WORDS:].bitcast(U8),
+                    in_=v_grouped[hd][:, g].rearrange("p w t -> p (w t)"),
+                )
+            for j, host in enumerate(HOSTS):
+                own = (host + 1) * QUADRANT - P
+                nc.sync.dma_start(
+                    out=v_shared[0:own, hd % 2, j, 0, :].bitcast(I32),
+                    in_=v_blocks[0:own, hd, 1, :].bitcast(I32),
+                )
+                nc.sync.dma_start(
+                    out=v_shared[own:P, hd % 2, j, 1, :].bitcast(I32),
+                    in_=v_blocks[0 : P - own, hd, 0, :].bitcast(I32),
+                )
 
         heads = {}
 
@@ -232,8 +260,7 @@ def tile_retentivenetwork_pa_kernel(tc, q, k, v, theta, out):
             )
             nc.vector.tensor_copy(out=neg_weight[:, cols], in_=table_ps[:, :width])
 
-        units = [(hd, i) for hd in range(HEADS - 1) for i in range(NT)]
-        units.extend([(HEADS - 1, i) for i in reversed(range(NT))])
+        units = [(hd, i) for hd in range(HEADS) for i in ORDER]
         live = {}
 
         def scores(u):
@@ -245,7 +272,7 @@ def tile_retentivenetwork_pa_kernel(tc, q, k, v, theta, out):
                     load_head(hd + 2)
                 if hd == 4:
                     load_values(1)
-            if i == 1 and hd + 1 < HEADS:
+            if u % NT == 1 and hd + 1 < HEADS:
                 regroup_values(hd + 1)
             keys = (i + 1) * P
             banks = []
@@ -270,16 +297,16 @@ def tile_retentivenetwork_pa_kernel(tc, q, k, v, theta, out):
                     )
                 banks.append((k0, width, bank))
             live[u] = {"banks": banks}
-            if hd + 1 < HEADS and i == TRANSPOSE_Q_AFTER:
+            if hd + 1 < HEADS and u % NT == TRANSPOSE_Q_AFTER:
                 transpose_rows(hd + 1, "q")
-            if hd + 1 < HEADS and i == TRANSPOSE_K_AFTER:
+            if hd + 1 < HEADS and u % NT == TRANSPOSE_K_AFTER:
                 transpose_rows(hd + 1, "k")
 
         def next_head_rows(u):
             hd, i = units[u]
-            if hd + 1 < HEADS and i == TRANSPOSE_Q_AFTER:
+            if hd + 1 < HEADS and u % NT == TRANSPOSE_Q_AFTER:
                 collect_rows(hd + 1, "q")
-            if hd + 1 < HEADS and i == TRANSPOSE_K_AFTER:
+            if hd + 1 < HEADS and u % NT == TRANSPOSE_K_AFTER:
                 collect_rows(hd + 1, "k")
 
         def weigh(u):
@@ -297,8 +324,10 @@ def tile_retentivenetwork_pa_kernel(tc, q, k, v, theta, out):
 
         def row_maximum(u):
             hd, i = units[u]
+            bank, slot = column_of(i)
+            live[u]["column"] = 4 * bank + slot
             nc.vector.tensor_reduce(
-                out=heads[hd]["neg_max"][:, i : i + 1],
+                out=heads[hd]["neg_max"][:, 4 * bank + slot : 4 * bank + slot + 1],
                 in_=live[u]["neg_s"][:, : (i + 1) * P],
                 axis=AXIS.X,
                 op=ALU.min,
@@ -307,17 +336,22 @@ def tile_retentivenetwork_pa_kernel(tc, q, k, v, theta, out):
         def exponentials(u):
             hd, i = units[u]
             keys = (i + 1) * P
+            column = live[u]["column"]
+            home = 6 - i if i in RIDERS else i
+            first = (home + 1) * QUADRANT if i in RIDERS else 0
             nc.scalar.activation(
-                out=e_tiles[(i, hd % 2)][:, :, 0 : keys // PACK, :],
+                out=e_tiles[(home, hd % 2)][:, :, first : first + keys // PACK, :],
                 in_=live[u]["neg_s"][:, :keys].rearrange("q (a u e) -> q u a e", u=2, e=2),
                 func=FUNC.Exp,
-                bias=heads[hd]["neg_max"][:, i : i + 1],
+                bias=heads[hd]["neg_max"][:, column : column + 1],
                 scale=-1.0,
-                accum_out=heads[hd]["row_sum"][:, i : i + 1],
+                accum_out=heads[hd]["row_sum"][:, column : column + 1],
             )
 
         def transposes(u):
             hd, i = units[u]
+            if i in RIDERS:
+                return
             passes = passes_of(i)
             e_words = e_tiles[(i, hd % 2)][:].rearrange("q u a e -> q (u a e)").bitcast(F32)
             words_ps = ps_words.tile([P, passes, 2, P], F32, name="words_ps")
@@ -329,6 +363,8 @@ def tile_retentivenetwork_pa_kernel(tc, q, k, v, theta, out):
 
         def regroup(u):
             hd, i = units[u]
+            if i in RIDERS:
+                return
             passes = passes_of(i)
             grouped = work.tile([P, passes * K_PASS], BF16, name="e_grouped", align_bytes=64)
             nc.scalar.copy(
@@ -339,10 +375,10 @@ def tile_retentivenetwork_pa_kernel(tc, q, k, v, theta, out):
 
         def quantise(u):
             hd, i = units[u]
-            if u == 0:
-                quantise_values(0)
-            if i == 4 and hd + 1 < HEADS:
+            if u % NT == 4 and hd + 1 < HEADS:
                 quantise_values(hd + 1)
+            if i in RIDERS:
+                return
             passes = passes_of(i)
             codes = work.tile([P, passes * P], U32, name="e_codes", align_bytes=64)
             scales = work.tile([P, passes * P], U8, name="e_scales", align_bytes=64)
@@ -350,51 +386,69 @@ def tile_retentivenetwork_pa_kernel(tc, q, k, v, theta, out):
             live[u]["codes"] = codes
             live[u]["scales"] = scales
 
+        def multiply(hd, i, codes, scales, g, block, start, stop):
+            bank, slot = column_of(i)
+            nc.tensor.matmul_mx(
+                out=heads[hd][("acc", bank)][:, slot, :],
+                lhsT=codes[:, g * P : (g + 1) * P].bitcast(FP8X4),
+                lhsT_scale=scales[:, g * P : (g + 1) * P],
+                rhs=block[:, :CODE_WORDS].bitcast(FP8X4),
+                rhs_scale=block[:, CODE_WORDS:].bitcast(U8),
+                start=start,
+                stop=stop,
+            )
+
         def multiply_values(u):
             hd, i = units[u]
-            b, h = divmod(hd, H)
-            if u % 4 == 0:
-                heads[hd]["acc"] = ps_out.tile([P, 4, HD], F32, name="acc")
-            passes = passes_of(i)
-            for g in range(passes):
-                nc.tensor.matmul_mx(
-                    out=heads[hd]["acc"][:, i % 4, :],
-                    lhsT=live[u]["codes"][:, g * P : (g + 1) * P].bitcast(FP8X4),
-                    lhsT_scale=live[u]["scales"][:, g * P : (g + 1) * P],
-                    rhs=v_codes[:, hd, g, :].bitcast(FP8X4),
-                    rhs_scale=v_scales[:, hd, g, :],
-                    start=(g == 0),
-                    stop=(g == passes - 1),
-                )
-            live[u]["acc"] = heads[hd]["acc"]
+            if i in RIDERS:
+                return
+            for bank in range(2):
+                if i == [t for t in ORDER if t in BANK_TILES[bank] and t not in RIDERS][0]:
+                    heads[hd][("acc", bank)] = ps_out.tile([P, 4, HD], F32, name="acc")
+            codes, scales = live[u]["codes"], live[u]["scales"]
+            if i in HOSTS:
+                j = HOSTS.index(i)
+                multiply(hd, i, codes, scales, 0, v_blocks[:, hd, 0, :], True, False)
+                multiply(hd, i, codes, scales, 1, v_shared[:, hd % 2, j, 0, :], False, True)
+                multiply(hd, 6 - i, codes, scales, 1, v_shared[:, hd % 2, j, 1, :], True, True)
+            else:
+                passes = passes_of(i)
+                for g in range(passes):
+                    multiply(hd, i, codes, scales, g, v_blocks[:, hd, g, :], g == 0, g == passes - 1)
 
         def store(u):
             hd, i = units[u]
             b, h = divmod(hd, H)
-            if u % 4 != 3:
+            if i not in BANK_FULL_AFTER:
                 return
-            first = i - i % 4
+            bank = BANK_FULL_AFTER.index(i)
             inverse = stat_pool.tile([P, 4], F32, name="inverse")
             nc.gpsimd.tensor_tensor(
-                out=inverse[:], in0=heads[hd]["row_sum"][:, first : first + 4], in1=minus_one[:], op=ALU.pow
+                out=inverse[:],
+                in0=heads[hd]["row_sum"][:, 4 * bank : 4 * bank + 4],
+                in1=minus_one[:],
+                op=ALU.pow,
             )
             result = work.tile([P, 4, HD], F32, name="result")
             for s in range(4):
                 nc.scalar.activation(
                     out=result[:, s, :],
-                    in_=live[u]["acc"][:, s, :],
+                    in_=heads[hd][("acc", bank)][:, s, :],
                     func=FUNC.Copy,
                     scale=inverse[:, s : s + 1],
                 )
-            nc.sync.dma_start(
-                out=out[b, first * P : (first + 4) * P, h, :].rearrange("(s p) d -> p s d", p=P),
-                in_=result[:],
-            )
+            for s in (0, 2):
+                first = BANK_TILES[bank][s]
+                nc.sync.dma_start(
+                    out=out[b, first * P : (first + 2) * P, h, :].rearrange("(s p) d -> p s d", p=P),
+                    in_=result[:, s : s + 2, :],
+                )
 
         def run(stage, u):
             if 0 <= u < len(units):
                 stage(u)
 
+        quantise_values(0)
         scores(0)
         for step in range(len(units) + LAG_STORE):
             run(transposes, step - LAG_TRANSPOSE)

@@ -153,8 +153,7 @@ def tile_retentivenetwork_pa_kernel(tc, q, k, v, theta, out):
             b, h = divmod(hd, H)
             grouped = value_pool.tile([P, T // K_PASS, HD, PACK], BF16, name="v_grouped", align_bytes=64)
             for g in range(T // K_PASS):
-                copy = nc.vector.tensor_copy if g == 0 else nc.scalar.copy
-                copy(
+                nc.scalar.copy(
                     out=grouped[:, g].rearrange("p (c r) t -> p c t r", r=4),
                     in_=v_raw[(b, g)][:, :, h * HD : (h + 1) * HD].rearrange("p t (c r) -> p c t r", r=4),
                 )

@@ -41,7 +41,7 @@ RIDERS = (0, 1, 2)
 HOSTS = (4, 5, 6)
 QUADRANT = 32
 BANK_TILES = ((0, 1, 6, 7), (2, 3, 4, 5))
-BANK_FULL_AFTER = (5, 3)
+FIRST_ORDER = (3, 2, 4, 1, 5, 0, 6, 7)
 CODE_WORDS = HD
 BLOCK_WORDS = HD + HD // 4
 
@@ -55,12 +55,24 @@ def column_of(i):
     return bank, BANK_TILES[bank].index(i)
 
 
+def bank_plan(order):
+    opened, filled = {}, {}
+    for i in order:
+        if i in RIDERS:
+            continue
+        for tile in (i, 6 - i) if i in HOSTS else (i,):
+            bank = column_of(tile)[0]
+            opened.setdefault(bank, i)
+            filled[bank] = i
+    return opened, filled
+
+
 def tile_retentivenetwork_pa_kernel(tc, q, k, v, theta, out):
     nc = tc.nc
     with ExitStack() as ctx:
         const = ctx.enter_context(tc.tile_pool(name="const", bufs=1))
         table_pool = ctx.enter_context(tc.tile_pool(name="table", bufs=3))
-        value_pool = ctx.enter_context(tc.tile_pool(name="values", bufs=2))
+        value_pool = ctx.enter_context(tc.tile_pool(name="values", bufs=4))
         raw_pool = ctx.enter_context(tc.tile_pool(name="raw", bufs=3))
         cols_pool = ctx.enter_context(tc.tile_pool(name="cols", bufs=2))
         stat_pool = ctx.enter_context(tc.tile_pool(name="stats", bufs=3))
@@ -153,10 +165,21 @@ def tile_retentivenetwork_pa_kernel(tc, q, k, v, theta, out):
             b, h = divmod(hd, H)
             grouped = value_pool.tile([P, T // K_PASS, HD, PACK], BF16, name="v_grouped", align_bytes=64)
             for g in range(T // K_PASS):
-                nc.scalar.copy(
-                    out=grouped[:, g].rearrange("p (c r) t -> p c t r", r=4),
-                    in_=v_raw[(b, g)][:, :, h * HD : (h + 1) * HD].rearrange("p t (c r) -> p c t r", r=4),
-                )
+                if hd < 2:
+                    nc.scalar.copy(
+                        out=grouped[:, g].rearrange("p (c r) t -> p c t r", r=4),
+                        in_=v_raw[(b, g)][:, :, h * HD : (h + 1) * HD].rearrange("p t (c r) -> p c t r", r=4),
+                    )
+                    continue
+                for c0 in range(0, HD, HD // 2):
+                    nc.gpsimd.tensor_scalar(
+                        out=grouped[:, g, c0 : c0 + HD // 2, :],
+                        in0=v_raw[(b, g)][:, :, h * HD + c0 : h * HD + c0 + HD // 2].rearrange("p t c -> p c t"),
+                        scalar1=1.0,
+                        scalar2=0.0,
+                        op0=ALU.mult,
+                        op1=ALU.add,
+                    )
             v_grouped[hd] = grouped
 
         def quantise_values(hd):
@@ -204,7 +227,6 @@ def tile_retentivenetwork_pa_kernel(tc, q, k, v, theta, out):
         load_head(0)
         load_values(0)
         load_head(1)
-        regroup_values(0)
 
         neg_weight = const.tile([P, T], F32)
         by_query = const.tile([P, P], F32)
@@ -259,7 +281,8 @@ def tile_retentivenetwork_pa_kernel(tc, q, k, v, theta, out):
             )
             nc.vector.tensor_copy(out=neg_weight[:, cols], in_=table_ps[:, :width])
 
-        units = [(hd, i) for hd in range(HEADS) for i in ORDER]
+        orders = [FIRST_ORDER if hd == 0 else ORDER for hd in range(HEADS)]
+        units = [(hd, i) for hd in range(HEADS) for i in orders[hd]]
         live = {}
 
         def scores(u):
@@ -271,8 +294,10 @@ def tile_retentivenetwork_pa_kernel(tc, q, k, v, theta, out):
                     load_head(hd + 2)
                 if hd == 4:
                     load_values(1)
-            if u % NT == 1 and hd + 1 < HEADS:
-                regroup_values(hd + 1)
+            if u in (1, 3):
+                regroup_values(u // 2)
+            if u % NT == 5 and hd + 2 < HEADS:
+                regroup_values(hd + 2)
             keys = (i + 1) * P
             banks = []
             for k0 in range(0, keys, BANK):
@@ -402,7 +427,7 @@ def tile_retentivenetwork_pa_kernel(tc, q, k, v, theta, out):
             if i in RIDERS:
                 return
             for bank in range(2):
-                if i == [t for t in ORDER if t in BANK_TILES[bank] and t not in RIDERS][0]:
+                if i == bank_plan(orders[hd])[0][bank]:
                     heads[hd][("acc", bank)] = ps_out.tile([P, 4, HD], F32, name="acc")
             codes, scales = live[u]["codes"], live[u]["scales"]
             if i in HOSTS:
@@ -418,9 +443,10 @@ def tile_retentivenetwork_pa_kernel(tc, q, k, v, theta, out):
         def store(u):
             hd, i = units[u]
             b, h = divmod(hd, H)
-            if i not in BANK_FULL_AFTER:
+            filled = bank_plan(orders[hd])[1]
+            if i not in (filled[0], filled[1]):
                 return
-            bank = BANK_FULL_AFTER.index(i)
+            bank = 0 if i == filled[0] else 1
             inverse = stat_pool.tile([P, 4], F32, name="inverse")
             nc.gpsimd.tensor_tensor(
                 out=inverse[:],
@@ -447,9 +473,10 @@ def tile_retentivenetwork_pa_kernel(tc, q, k, v, theta, out):
             if 0 <= u < len(units):
                 stage(u)
 
-        quantise_values(0)
         scores(0)
         for step in range(len(units) + LAG_STORE):
+            if step == 2:
+                quantise_values(0)
             run(transposes, step - LAG_TRANSPOSE)
             run(multiply_values, step - LAG_MULTIPLY)
             run(scores, step + 1)

@@ -36,12 +36,14 @@ TRANSPOSE_Q_AFTER = 2
 TRANSPOSE_K_AFTER = 5
 
 
-ORDER = (7, 0, 6, 1, 5, 2, 4, 3)
+ORDER = (2, 4, 1, 5, 0, 6, 3, 7)
 RIDERS = (0, 1, 2)
 HOSTS = (4, 5, 6)
 QUADRANT = 32
 BANK_TILES = ((0, 1, 6, 7), (2, 3, 4, 5))
 FIRST_ORDER = (3, 2, 4, 1, 5, 0, 6, 7)
+LAST_ORDER = (2, 4, 7, 1, 5, 0, 6, 3)
+EARLY = (7,)
 CODE_WORDS = HD
 BLOCK_WORDS = HD + HD // 4
 
@@ -78,6 +80,8 @@ def tile_retentivenetwork_pa_kernel(tc, q, k, v, theta, out):
         stat_pool = ctx.enter_context(tc.tile_pool(name="stats", bufs=3))
         work = ctx.enter_context(tc.tile_pool(name="work", bufs=3))
         score_pool = ctx.enter_context(tc.tile_pool(name="neg_s", bufs=5))
+        early_pool = ctx.enter_context(tc.tile_pool(name="neg_s_early", bufs=2))
+        raw_score_pool = ctx.enter_context(tc.tile_pool(name="raw_scores", bufs=2))
         ps_scores = ctx.enter_context(tc.psum_pool(name="ps_scores", bufs=4))
         ps_words = ctx.enter_context(tc.psum_pool(name="ps_words", bufs=2))
         ps_out = ctx.enter_context(tc.psum_pool(name="ps_out", bufs=2))
@@ -281,9 +285,32 @@ def tile_retentivenetwork_pa_kernel(tc, q, k, v, theta, out):
             )
             nc.vector.tensor_copy(out=neg_weight[:, cols], in_=table_ps[:, :width])
 
-        orders = [FIRST_ORDER if hd == 0 else ORDER for hd in range(HEADS)]
+        orders = [FIRST_ORDER] + [ORDER] * (HEADS - 2) + [LAST_ORDER]
         units = [(hd, i) for hd in range(HEADS) for i in orders[hd]]
         live = {}
+
+        def early_scores(hd):
+            for i in EARLY:
+                bank = ps_scores.tile([P, BANK], F32, name="scores_ps")
+                nc.tensor.matmul(
+                    out=bank[:],
+                    lhsT=heads[hd]["q"][:, i * P : (i + 1) * P],
+                    rhs=heads[hd]["k"][:, 0:BANK],
+                    start=True,
+                    stop=True,
+                )
+                raw_scores = raw_score_pool.tile([P, BANK], F32, name="raw_scores")
+                nc.scalar.copy(out=raw_scores[:], in_=bank[:])
+                neg_s = early_pool.tile([P, T], F32, name="neg_s_early_%d" % i)
+                first = T - (i + 1) * P
+                for c0 in range(0, BANK, BANK // 2):
+                    nc.gpsimd.tensor_tensor(
+                        out=neg_s[:, c0 : c0 + BANK // 2],
+                        in0=raw_scores[:, c0 : c0 + BANK // 2],
+                        in1=neg_weight[:, first + c0 : first + c0 + BANK // 2],
+                        op=ALU.mult,
+                    )
+                heads[hd][("early", i)] = neg_s
 
         def scores(u):
             hd, i = units[u]
@@ -300,7 +327,7 @@ def tile_retentivenetwork_pa_kernel(tc, q, k, v, theta, out):
                 regroup_values(hd + 2)
             keys = (i + 1) * P
             banks = []
-            for k0 in range(0, keys, BANK):
+            for k0 in range(BANK if i in EARLY else 0, keys, BANK):
                 width = min(BANK, keys - k0)
                 diagonal = k0 + width == keys
                 bank = ps_scores.tile([P, BANK], F32, name="scores_ps")
@@ -325,6 +352,8 @@ def tile_retentivenetwork_pa_kernel(tc, q, k, v, theta, out):
                 transpose_rows(hd + 1, "q")
             if hd + 1 < HEADS and u % NT == TRANSPOSE_K_AFTER:
                 transpose_rows(hd + 1, "k")
+            if hd + 1 < HEADS and u % NT == NT - 1:
+                early_scores(hd + 1)
 
         def next_head_rows(u):
             hd, i = units[u]
@@ -336,7 +365,10 @@ def tile_retentivenetwork_pa_kernel(tc, q, k, v, theta, out):
         def weigh(u):
             hd, i = units[u]
             keys = (i + 1) * P
-            neg_s = score_pool.tile([P, T], F32, name="neg_s")
+            if i in EARLY:
+                neg_s = heads[hd][("early", i)]
+            else:
+                neg_s = score_pool.tile([P, T], F32, name="neg_s")
             for k0, width, bank in live[u]["banks"]:
                 nc.vector.tensor_tensor(
                     out=neg_s[:, k0 : k0 + width],
@@ -473,6 +505,7 @@ def tile_retentivenetwork_pa_kernel(tc, q, k, v, theta, out):
             if 0 <= u < len(units):
                 stage(u)
 
+        early_scores(0)
         scores(0)
         for step in range(len(units) + LAG_STORE):
             if step == 2:

@@ -43,7 +43,8 @@ QUADRANT = 32
 BANK_TILES = ((0, 1, 6, 7), (2, 3, 4, 5))
 FIRST_ORDER = (3, 2, 4, 1, 5, 0, 6, 7)
 LAST_ORDER = (2, 4, 7, 1, 5, 0, 6, 3)
-EARLY = (7,)
+EARLY_KEYS = {7: 512}
+LAG_RECIPROCAL = 2
 CODE_WORDS = HD
 BLOCK_WORDS = HD + HD // 4
 
@@ -175,10 +176,10 @@ def tile_retentivenetwork_pa_kernel(tc, q, k, v, theta, out):
                         in_=v_raw[(b, g)][:, :, h * HD : (h + 1) * HD].rearrange("p t (c r) -> p c t r", r=4),
                     )
                     continue
-                for c0 in range(0, HD, HD // 2):
+                for c0 in range(0, HD, HD // 4):
                     nc.gpsimd.tensor_scalar(
-                        out=grouped[:, g, c0 : c0 + HD // 2, :],
-                        in0=v_raw[(b, g)][:, :, h * HD + c0 : h * HD + c0 + HD // 2].rearrange("p t c -> p c t"),
+                        out=grouped[:, g, c0 : c0 + HD // 4, :],
+                        in0=v_raw[(b, g)][:, :, h * HD + c0 : h * HD + c0 + HD // 4].rearrange("p t c -> p c t"),
                         scalar1=1.0,
                         scalar2=0.0,
                         op0=ALU.mult,
@@ -289,28 +290,28 @@ def tile_retentivenetwork_pa_kernel(tc, q, k, v, theta, out):
         units = [(hd, i) for hd in range(HEADS) for i in orders[hd]]
         live = {}
 
-        def early_scores(hd):
-            for i in EARLY:
-                bank = ps_scores.tile([P, BANK], F32, name="scores_ps")
-                nc.tensor.matmul(
-                    out=bank[:],
-                    lhsT=heads[hd]["q"][:, i * P : (i + 1) * P],
-                    rhs=heads[hd]["k"][:, 0:BANK],
-                    start=True,
-                    stop=True,
+        def early_scores(hd, i):
+            width = EARLY_KEYS[i]
+            bank = ps_scores.tile([P, BANK], F32, name="scores_ps")
+            nc.tensor.matmul(
+                out=bank[:, :width],
+                lhsT=heads[hd]["q"][:, i * P : (i + 1) * P],
+                rhs=heads[hd]["k"][:, 0:width],
+                start=True,
+                stop=True,
+            )
+            raw_scores = raw_score_pool.tile([P, BANK], F32, name="raw_scores")
+            nc.scalar.copy(out=raw_scores[:, :width], in_=bank[:, :width])
+            neg_s = early_pool.tile([P, T], F32, name="neg_s_early_%d" % i)
+            first = T - (i + 1) * P
+            for c0 in range(0, width, P):
+                nc.gpsimd.tensor_tensor(
+                    out=neg_s[:, c0 : c0 + P],
+                    in0=raw_scores[:, c0 : c0 + P],
+                    in1=neg_weight[:, first + c0 : first + c0 + P],
+                    op=ALU.mult,
                 )
-                raw_scores = raw_score_pool.tile([P, BANK], F32, name="raw_scores")
-                nc.scalar.copy(out=raw_scores[:], in_=bank[:])
-                neg_s = early_pool.tile([P, T], F32, name="neg_s_early_%d" % i)
-                first = T - (i + 1) * P
-                for c0 in range(0, BANK, BANK // 2):
-                    nc.gpsimd.tensor_tensor(
-                        out=neg_s[:, c0 : c0 + BANK // 2],
-                        in0=raw_scores[:, c0 : c0 + BANK // 2],
-                        in1=neg_weight[:, first + c0 : first + c0 + BANK // 2],
-                        op=ALU.mult,
-                    )
-                heads[hd][("early", i)] = neg_s
+            heads[hd][("early", i)] = neg_s
 
         def scores(u):
             hd, i = units[u]
@@ -327,9 +328,11 @@ def tile_retentivenetwork_pa_kernel(tc, q, k, v, theta, out):
                 regroup_values(hd + 2)
             keys = (i + 1) * P
             banks = []
-            for k0 in range(BANK if i in EARLY else 0, keys, BANK):
-                width = min(BANK, keys - k0)
-                diagonal = k0 + width == keys
+            done = EARLY_KEYS.get(i, 0)
+            edges = [done] + [x for x in range(BANK, keys, BANK) if x > done] + [keys]
+            for k0, k1 in zip(edges[:-1], edges[1:]):
+                width = k1 - k0
+                diagonal = k1 == keys
                 bank = ps_scores.tile([P, BANK], F32, name="scores_ps")
                 nc.tensor.matmul(
                     out=bank[:, :width],
@@ -353,7 +356,7 @@ def tile_retentivenetwork_pa_kernel(tc, q, k, v, theta, out):
             if hd + 1 < HEADS and u % NT == TRANSPOSE_K_AFTER:
                 transpose_rows(hd + 1, "k")
             if hd + 1 < HEADS and u % NT == NT - 1:
-                early_scores(hd + 1)
+                early_scores(hd + 1, 7)
 
         def next_head_rows(u):
             hd, i = units[u]
@@ -365,7 +368,7 @@ def tile_retentivenetwork_pa_kernel(tc, q, k, v, theta, out):
         def weigh(u):
             hd, i = units[u]
             keys = (i + 1) * P
-            if i in EARLY:
+            if i in EARLY_KEYS:
                 neg_s = heads[hd][("early", i)]
             else:
                 neg_s = score_pool.tile([P, T], F32, name="neg_s")
@@ -472,6 +475,19 @@ def tile_retentivenetwork_pa_kernel(tc, q, k, v, theta, out):
                 for g in range(passes):
                     multiply(hd, i, codes, scales, g, v_blocks[:, hd, g, :], g == 0, g == passes - 1)
 
+        def reciprocals(u):
+            hd, i = units[u]
+            for bank in range(2):
+                if i == [t for t in orders[hd] if t in BANK_TILES[bank]][-1]:
+                    inverse = stat_pool.tile([P, 4], F32, name="inverse")
+                    nc.gpsimd.tensor_tensor(
+                        out=inverse[:],
+                        in0=heads[hd]["row_sum"][:, 4 * bank : 4 * bank + 4],
+                        in1=minus_one[:],
+                        op=ALU.pow,
+                    )
+                    heads[hd][("inverse", bank)] = inverse
+
         def store(u):
             hd, i = units[u]
             b, h = divmod(hd, H)
@@ -479,13 +495,7 @@ def tile_retentivenetwork_pa_kernel(tc, q, k, v, theta, out):
             if i not in (filled[0], filled[1]):
                 return
             bank = 0 if i == filled[0] else 1
-            inverse = stat_pool.tile([P, 4], F32, name="inverse")
-            nc.gpsimd.tensor_tensor(
-                out=inverse[:],
-                in0=heads[hd]["row_sum"][:, 4 * bank : 4 * bank + 4],
-                in1=minus_one[:],
-                op=ALU.pow,
-            )
+            inverse = heads[hd][("inverse", bank)]
             result = work.tile([P, 4, HD], F32, name="result")
             for s in range(4):
                 nc.scalar.activation(
@@ -505,7 +515,7 @@ def tile_retentivenetwork_pa_kernel(tc, q, k, v, theta, out):
             if 0 <= u < len(units):
                 stage(u)
 
-        early_scores(0)
+        early_scores(0, 7)
         scores(0)
         for step in range(len(units) + LAG_STORE):
             if step == 2:
@@ -514,6 +524,7 @@ def tile_retentivenetwork_pa_kernel(tc, q, k, v, theta, out):
             run(multiply_values, step - LAG_MULTIPLY)
             run(scores, step + 1)
             run(exponentials, step - LAG_EXP)
+            run(reciprocals, step - LAG_RECIPROCAL)
             run(regroup, step - LAG_REGROUP)
             run(next_head_rows, step)
             run(store, step - LAG_STORE)

from contextlib import ExitStack
import math

import concourse.mybir as mybir
from concourse.masks import make_identity

F32 = mybir.dt.float32
BF16 = mybir.dt.bfloat16
I32 = mybir.dt.int32
U32 = mybir.dt.uint32
U8 = mybir.dt.uint8
FP8X4 = mybir.dt.float8_e4m3fn_x4
ALU = mybir.AluOpType
FUNC = mybir.ActivationFunctionType
AXIS = mybir.AxisListType

B, T, H, HD = 2, 1024, 8, 128
P = 128
PACK = 4
K_PASS = P * PACK
BANK = 512
NT = T // P
HEADS = B * H
FLOPS = 4 * B * H * HD * (K_PASS * K_PASS + K_PASS * T)

TABLE_SCALE = -1.0 / (H * math.sqrt(HD))
SHUT_OUT = -(2.0 ** 100)

LAG_EXP = 1
LAG_TRANSPOSE = 3
LAG_REGROUP = 4
LAG_QUANTISE = 5
LAG_MULTIPLY = 6
LAG_STORE = 7
TRANSPOSE_Q_AFTER = 2
TRANSPOSE_K_AFTER = 5


ORDER = (2, 4, 1, 5, 0, 6, 3, 7)
RIDERS = (0, 1, 2)
HOSTS = (4, 5, 6)
QUADRANT = 32
BANK_TILES = ((0, 1, 6, 7), (2, 3, 4, 5))
FIRST_ORDER = (3, 2, 4, 1, 5, 0, 6, 7)
LAST_ORDER = (2, 4, 7, 1, 5, 0, 6, 3)
EARLY_KEYS = {7: 512}
LAG_RECIPROCAL = 2
CODE_WORDS = HD
BLOCK_WORDS = HD + HD // 4


def passes_of(i):
    return (i * P) // K_PASS + 1


def column_of(i):
    bank = 0 if i in BANK_TILES[0] else 1
    return bank, BANK_TILES[bank].index(i)


def bank_plan(order):
    opened, filled = {}, {}
    for i in order:
        if i in RIDERS:
            continue
        for tile in (i, 6 - i) if i in HOSTS else (i,):
            bank = column_of(tile)[0]
            opened.setdefault(bank, i)
            filled[bank] = i
    return opened, filled


def tile_retentivenetwork_pa_kernel(tc, q, k, v, theta, out):
    nc = tc.nc
    with ExitStack() as ctx:
        const = ctx.enter_context(tc.tile_pool(name="const", bufs=1))
        table_pool = ctx.enter_context(tc.tile_pool(name="table", bufs=3))
        value_pool = ctx.enter_context(tc.tile_pool(name="values", bufs=4))
        raw_pool = ctx.enter_context(tc.tile_pool(name="raw", bufs=3))
        cols_pool = ctx.enter_context(tc.tile_pool(name="cols", bufs=2))
        stat_pool = ctx.enter_context(tc.tile_pool(name="stats", bufs=3))
        work = ctx.enter_context(tc.tile_pool(name="work", bufs=3))
        score_pool = ctx.enter_context(tc.tile_pool(name="neg_s", bufs=5))
        early_pool = ctx.enter_context(tc.tile_pool(name="neg_s_early", bufs=2))
        raw_score_pool = ctx.enter_context(tc.tile_pool(name="raw_scores", bufs=2))
        ps_scores = ctx.enter_context(tc.psum_pool(name="ps_scores", bufs=4))
        ps_words = ctx.enter_context(tc.psum_pool(name="ps_words", bufs=2))
        ps_out = ctx.enter_context(tc.psum_pool(name="ps_out", bufs=2))

        theta_bf = const.tile([P, H], BF16)
        nc.sync.dma_start(out=theta_bf[:], in_=theta.partition_broadcast(P))

        distance = const.tile([P, P], F32)
        nc.gpsimd.iota(
            distance[:],
            pattern=[[-1, P]],
            base=0,
            channel_multiplier=1,
            allow_small_or_imprecise_dtypes=True,
        )
        ident_f32 = const.tile([P, P], F32)
        make_identity(nc, ident_f32[:])
        ident_bf = const.tile([P, P], BF16)
        make_identity(nc, ident_bf[:])
        upward = const.tile([P, P], F32)
        nc.gpsimd.iota(
            upward[:], pattern=[[1, P]], base=0, channel_multiplier=0, allow_small_or_imprecise_dtypes=True
        )
        backward = const.tile([P, T - P], F32)
        nc.gpsimd.iota(
            backward[:],
            pattern=[[-1, T - P]],
            base=T - P,
            channel_multiplier=0,
            allow_small_or_imprecise_dtypes=True,
        )

        shut_out = const.tile([P, P], BF16)
        nc.vector.tensor_scalar(
            out=shut_out[:],
            in0=distance[:],
            scalar1=0.0,
            scalar2=SHUT_OUT,
            op0=ALU.is_lt,
            op1=ALU.mult,
        )
        nc.vector.tensor_scalar_max(out=distance[:], in0=distance[:], scalar1=0.0)
        minus_one = const.tile([P, 4], F32)
        nc.gpsimd.memset(minus_one[:], -1.0)
        neg_theta = const.tile([P, H], F32)
        nc.vector.tensor_scalar_mul(out=neg_theta[:], in0=theta_bf[:], scalar1=-1.0)
        on_diagonal = const.tile([P, H], F32)
        nc.vector.tensor_tensor(out=on_diagonal[:], in0=neg_theta[:], in1=ident_f32[:, 0:H], op=ALU.mult)
        neg_rate = const.tile([P, 1], F32)
        nc.vector.tensor_reduce(out=neg_rate[:], in_=on_diagonal[:], axis=AXIS.X, op=ALU.add)
        is_rate = const.tile([P, 1], F32)
        nc.vector.tensor_reduce(out=is_rate[:], in_=ident_f32[:, 0:H], axis=AXIS.X, op=ALU.add)

        e_tiles = {}
        for i in range(NT):
            if i in RIDERS:
                continue
            for parity in range(2):
                e_tiles[(i, parity)] = const.tile(
                    [P, 2, passes_of(i) * P, 2], BF16, name="e_%d_%d" % (i, parity)
                )

        v_blocks = const.tile([P, HEADS, T // K_PASS, BLOCK_WORDS], U32, align_bytes=64)
        nc.vector.memset(
            v_blocks[:].rearrange("p h g w -> p (h g) w")[:, :, CODE_WORDS:].bitcast(I32), 0
        )
        v_shared = const.tile([P, 2, len(HOSTS), 2, BLOCK_WORDS], U32, align_bytes=64)
        nc.vector.memset(v_shared[:].rearrange("p s j b w -> p (s j b w)").bitcast(I32), 0)
        v_raw = {}

        def load_values(b):
            for g in range(T // K_PASS):
                raw = const.tile([P, PACK, H * HD], BF16, name="v_raw_%d_%d" % (b, g))
                nc.sync.dma_start(
                    out=raw[:],
                    in_=v[b, g * K_PASS : (g + 1) * K_PASS].rearrange(
                        "(p t) h d -> p t (h d)", t=PACK
                    ),
                )
                v_raw[(b, g)] = raw

        v_grouped = {}

        def regroup_values(hd):
            b, h = divmod(hd, H)
            grouped = value_pool.tile([P, T // K_PASS, HD, PACK], BF16, name="v_grouped", align_bytes=64)
            for g in range(T // K_PASS):
                if hd < 2:
                    nc.scalar.copy(
                        out=grouped[:, g].rearrange("p (c r) t -> p c t r", r=4),
                        in_=v_raw[(b, g)][:, :, h * HD : (h + 1) * HD].rearrange("p t (c r) -> p c t r", r=4),
                    )
                    continue
                for c0 in range(0, HD, HD // 4):
                    nc.gpsimd.tensor_scalar(
                        out=grouped[:, g, c0 : c0 + HD // 4, :],
                        in0=v_raw[(b, g)][:, :, h * HD + c0 : h * HD + c0 + HD // 4].rearrange("p t c -> p c t"),
                        scalar1=1.0,
                        scalar2=0.0,
                        op0=ALU.mult,
                        op1=ALU.add,
                    )
            v_grouped[hd] = grouped

        def quantise_values(hd):
            for g in range(T // K_PASS):
                nc.vector.quantize_mx(
                    out=v_blocks[:, hd, g, :CODE_WORDS].bitcast(FP8X4),
                    scales=v_blocks[:, hd, g, CODE_WORDS:].bitcast(U8),
                    in_=v_grouped[hd][:, g].rearrange("p w t -> p (w t)"),
                )
            for j, host in enumerate(HOSTS):
                own = (host + 1) * QUADRANT - P
                nc.sync.dma_start(
                    out=v_shared[0:own, hd % 2, j, 0, :].bitcast(I32),
                    in_=v_blocks[0:own, hd, 1, :].bitcast(I32),
                )
                nc.sync.dma_start(
                    out=v_shared[own:P, hd % 2, j, 1, :].bitcast(I32),
                    in_=v_blocks[0 : P - own, hd, 0, :].bitcast(I32),
                )

        heads = {}

        def load_head(hd):
            b, h = divmod(hd, H)
            q_raw = raw_pool.tile([P, NT, HD], BF16, name="q_raw")
            nc.sync.dma_start(out=q_raw[:], in_=q[b, :, h, :].rearrange("(n p) d -> p n d", p=P))
            k_raw = raw_pool.tile([P, NT, HD], BF16, name="k_raw")
            nc.sync.dma_start(out=k_raw[:], in_=k[b, :, h, :].rearrange("(n p) d -> p n d", p=P))
            heads[hd] = {"q_raw": q_raw, "k_raw": k_raw}

        def transpose_rows(hd, which):
            rows_ps = ps_words.tile([P, NT, P], BF16, name="words_ps")
            for n in range(NT):
                nc.tensor.transpose(rows_ps[:, n, :], heads[hd][which + "_raw"][:, n, :], ident_bf[:])
            heads[hd][which + "_ps"] = rows_ps

        def collect_rows(hd, which, copy=nc.scalar.copy):
            channels = cols_pool.tile([P, T], BF16, name=which + "_channels")
            copy(
                out=channels[:].bitcast(F32),
                in_=heads[hd][which + "_ps"][:].rearrange("d n p -> d (n p)").bitcast(F32),
            )
            heads[hd][which] = channels

        load_head(0)
        load_values(0)
        load_head(1)

        neg_weight = const.tile([P, T], F32)
        by_query = const.tile([P, P], F32)
        nc.scalar.activation(out=by_query[:], in_=upward[:], func=FUNC.Exp, scale=neg_rate[:, 0:1])
        by_query_scaled = const.tile([P, P], F32)
        nc.vector.tensor_scalar(
            out=by_query_scaled[:],
            in0=by_query[:],
            scalar1=is_rate[:, 0:1],
            scalar2=TABLE_SCALE,
            op0=ALU.mult,
            op1=ALU.mult,
        )
        by_key = const.tile([P, T - P], F32)
        near, far = slice(BANK, T - P), slice(0, BANK)
        nc.scalar.activation(
            out=by_key[:, near], in_=backward[:, near], func=FUNC.Exp, scale=neg_rate[:, 0:1]
        )

        cols = slice(T - P, T)
        for c in range(H):
            decay = table_pool.tile([P, P], F32, name="decay")
            nc.scalar.activation(
                out=decay[:], in_=distance[:], func=FUNC.Exp, scale=neg_theta[:, c : c + 1]
            )
            if c == 0:
                nc.vector.tensor_scalar_mul(out=neg_weight[:, cols], in0=decay[:], scalar1=TABLE_SCALE)
            else:
                nc.vector.scalar_tensor_tensor(
                    out=neg_weight[:, cols],
                    in0=decay[:],
                    scalar=TABLE_SCALE,
                    in1=neg_weight[:, cols],
                    op0=ALU.mult,
                    op1=ALU.add,
                )

        transpose_rows(0, "q")
        transpose_rows(0, "k")
        collect_rows(0, "q")
        collect_rows(0, "k", nc.vector.tensor_copy)

        for cols in (near, far):
            width = cols.stop - cols.start
            if cols == far:
                nc.scalar.activation(
                    out=by_key[:, far], in_=backward[:, far], func=FUNC.Exp, scale=neg_rate[:, 0:1]
                )
            table_ps = ps_scores.tile([P, BANK], F32, name="scores_ps")
            nc.tensor.matmul(
                out=table_ps[:, :width], lhsT=by_query_scaled[:], rhs=by_key[:, cols], start=True, stop=True
            )
            nc.vector.tensor_copy(out=neg_weight[:, cols], in_=table_ps[:, :width])

        orders = [FIRST_ORDER] + [ORDER] * (HEADS - 2) + [LAST_ORDER]
        units = [(hd, i) for hd in range(HEADS) for i in orders[hd]]
        live = {}

        def early_scores(hd, i):
            width = EARLY_KEYS[i]
            bank = ps_scores.tile([P, BANK], F32, name="scores_ps")
            nc.tensor.matmul(
                out=bank[:, :width],
                lhsT=heads[hd]["q"][:, i * P : (i + 1) * P],
                rhs=heads[hd]["k"][:, 0:width],
                start=True,
                stop=True,
            )
            raw_scores = raw_score_pool.tile([P, BANK], F32, name="raw_scores")
            nc.scalar.copy(out=raw_scores[:, :width], in_=bank[:, :width])
            neg_s = early_pool.tile([P, T], F32, name="neg_s_early_%d" % i)
            first = T - (i + 1) * P
            for c0 in range(0, width, P):
                nc.gpsimd.tensor_tensor(
                    out=neg_s[:, c0 : c0 + P],
                    in0=raw_scores[:, c0 : c0 + P],
                    in1=neg_weight[:, first + c0 : first + c0 + P],
                    op=ALU.mult,
                )
            heads[hd][("early", i)] = neg_s

        def scores(u):
            hd, i = units[u]
            if u % NT == 0:
                heads[hd]["neg_max"] = stat_pool.tile([P, NT], F32, name="neg_max")
                heads[hd]["row_sum"] = stat_pool.tile([P, NT], F32, name="row_sum")
                if hd + 2 < HEADS:
                    load_head(hd + 2)
                if hd == 4:
                    load_values(1)
            if u in (1, 3):
                regroup_values(u // 2)
            if u % NT == 5 and hd + 2 < HEADS:
                regroup_values(hd + 2)
            keys = (i + 1) * P
            banks = []
            done = EARLY_KEYS.get(i, 0)
            edges = [done] + [x for x in range(BANK, keys, BANK) if x > done] + [keys]
            for k0, k1 in zip(edges[:-1], edges[1:]):
                width = k1 - k0
                diagonal = k1 == keys
                bank = ps_scores.tile([P, BANK], F32, name="scores_ps")
                nc.tensor.matmul(
                    out=bank[:, :width],
                    lhsT=heads[hd]["q"][:, i * P : (i + 1) * P],
                    rhs=heads[hd]["k"][:, k0 : k0 + width],
                    start=True,
                    stop=not diagonal,
                )
                if diagonal:
                    nc.tensor.matmul(
                        out=bank[:, width - P : width],
                        lhsT=ident_bf[:],
                        rhs=shut_out[:],
                        start=False,
                        stop=True,
                    )
                banks.append((k0, width, bank))
            live[u] = {"banks": banks}
            if hd + 1 < HEADS and u % NT == TRANSPOSE_Q_AFTER:
                transpose_rows(hd + 1, "q")
            if hd + 1 < HEADS and u % NT == TRANSPOSE_K_AFTER:
                transpose_rows(hd + 1, "k")
            if hd + 1 < HEADS and u % NT == NT - 1:
                early_scores(hd + 1, 7)

        def next_head_rows(u):
            hd, i = units[u]
            if hd + 1 < HEADS and u % NT == TRANSPOSE_Q_AFTER:
                collect_rows(hd + 1, "q")
            if hd + 1 < HEADS and u % NT == TRANSPOSE_K_AFTER:
                collect_rows(hd + 1, "k")

        def weigh(u):
            hd, i = units[u]
            keys = (i + 1) * P
            if i in EARLY_KEYS:
                neg_s = heads[hd][("early", i)]
            else:
                neg_s = score_pool.tile([P, T], F32, name="neg_s")
            for k0, width, bank in live[u]["banks"]:
                nc.vector.tensor_tensor(
                    out=neg_s[:, k0 : k0 + width],
                    in0=bank[:, :width],
                    in1=neg_weight[:, T - keys + k0 : T - keys + k0 + width],
                    op=ALU.mult,
                )
            live[u]["neg_s"] = neg_s

        def row_maximum(u):
            hd, i = units[u]
            bank, slot = column_of(i)
            live[u]["column"] = 4 * bank + slot
            nc.vector.tensor_reduce(
                out=heads[hd]["neg_max"][:, 4 * bank + slot : 4 * bank + slot + 1],
                in_=live[u]["neg_s"][:, : (i + 1) * P],
                axis=AXIS.X,
                op=ALU.min,
            )

        def exponentials(u):
            hd, i = units[u]
            keys = (i + 1) * P
            column = live[u]["column"]
            home = 6 - i if i in RIDERS else i
            first = (home + 1) * QUADRANT if i in RIDERS else 0
            nc.scalar.activation(
                out=e_tiles[(home, hd % 2)][:, :, first : first + keys // PACK, :],
                in_=live[u]["neg_s"][:, :keys].rearrange("q (a u e) -> q u a e", u=2, e=2),
                func=FUNC.Exp,
                bias=heads[hd]["neg_max"][:, column : column + 1],
                scale=-1.0,
                accum_out=heads[hd]["row_sum"][:, column : column + 1],
            )

        def transposes(u):
            hd, i = units[u]
            if i in RIDERS:
                return
            passes = passes_of(i)
            e_words = e_tiles[(i, hd % 2)][:].rearrange("q u a e -> q (u a e)").bitcast(F32)
            words_ps = ps_words.tile([P, passes, 2, P], F32, name="words_ps")
            for g in range(passes):
                for half in range(2):
                    first = half * passes * P + g * P
                    nc.tensor.transpose(words_ps[:, g, half, :], e_words[:, first : first + P], ident_f32[:])
            live[u]["words_ps"] = words_ps

        def regroup(u):
            hd, i = units[u]
            if i in RIDERS:
                return
            passes = passes_of(i)
            grouped = work.tile([P, passes * K_PASS], BF16, name="e_grouped", align_bytes=64)
            nc.scalar.copy(
                out=grouped[:].bitcast(F32).rearrange("p (g q u) -> p g q u", g=passes, u=2),
                in_=live[u]["words_ps"][:].rearrange("p g u q -> p g q u"),
            )
            live[u]["grouped"] = grouped

        def quantise(u):
            hd, i = units[u]
            if u % NT == 4 and hd + 1 < HEADS:
                quantise_values(hd + 1)
            if i in RIDERS:
                return
            passes = passes_of(i)
            codes = work.tile([P, passes * P], U32, name="e_codes", align_bytes=64)
            scales = work.tile([P, passes * P], U8, name="e_scales", align_bytes=64)
            nc.vector.quantize_mx(out=codes[:].bitcast(FP8X4), scales=scales[:], in_=live[u]["grouped"][:])
            live[u]["codes"] = codes
            live[u]["scales"] = scales

        def multiply(hd, i, codes, scales, g, block, start, stop):
            bank, slot = column_of(i)
            nc.tensor.matmul_mx(
                out=heads[hd][("acc", bank)][:, slot, :],
                lhsT=codes[:, g * P : (g + 1) * P].bitcast(FP8X4),
                lhsT_scale=scales[:, g * P : (g + 1) * P],
                rhs=block[:, :CODE_WORDS].bitcast(FP8X4),
                rhs_scale=block[:, CODE_WORDS:].bitcast(U8),
                start=start,
                stop=stop,
            )

        def multiply_values(u):
            hd, i = units[u]
            if i in RIDERS:
                return
            for bank in range(2):
                if i == bank_plan(orders[hd])[0][bank]:
                    heads[hd][("acc", bank)] = ps_out.tile([P, 4, HD], F32, name="acc")
            codes, scales = live[u]["codes"], live[u]["scales"]
            if i in HOSTS:
                j = HOSTS.index(i)
                multiply(hd, i, codes, scales, 0, v_blocks[:, hd, 0, :], True, False)
                multiply(hd, i, codes, scales, 1, v_shared[:, hd % 2, j, 0, :], False, True)
                multiply(hd, 6 - i, codes, scales, 1, v_shared[:, hd % 2, j, 1, :], True, True)
            else:
                passes = passes_of(i)
                for g in range(passes):
                    multiply(hd, i, codes, scales, g, v_blocks[:, hd, g, :], g == 0, g == passes - 1)

        def reciprocals(u):
            hd, i = units[u]
            for bank in range(2):
                if i == [t for t in orders[hd] if t in BANK_TILES[bank]][-1]:
                    inverse = stat_pool.tile([P, 4], F32, name="inverse")
                    nc.gpsimd.tensor_tensor(
                        out=inverse[:],
                        in0=heads[hd]["row_sum"][:, 4 * bank : 4 * bank + 4],
                        in1=minus_one[:],
                        op=ALU.pow,
                    )
                    heads[hd][("inverse", bank)] = inverse

        def store(u):
            hd, i = units[u]
            b, h = divmod(hd, H)
            filled = bank_plan(orders[hd])[1]
            if i not in (filled[0], filled[1]):
                return
            bank = 0 if i == filled[0] else 1
            inverse = heads[hd][("inverse", bank)]
            result = work.tile([P, 4, HD], F32, name="result")
            for s in range(4):
                nc.scalar.activation(
                    out=result[:, s, :],
                    in_=heads[hd][("acc", bank)][:, s, :],
                    func=FUNC.Copy,
                    scale=inverse[:, s : s + 1],
                )
            for s in (0, 2):
                first = BANK_TILES[bank][s]
                nc.sync.dma_start(
                    out=out[b, first * P : (first + 2) * P, h, :].rearrange("(s p) d -> p s d", p=P),
                    in_=result[:, s : s + 2, :],
                )

        def run(stage, u):
            if 0 <= u < len(units):
                stage(u)

        early_scores(0, 7)
        scores(0)
        for step in range(len(units) + LAG_STORE):
            if step == 2:
                quantise_values(0)
            run(transposes, step - LAG_TRANSPOSE)
            run(multiply_values, step - LAG_MULTIPLY)
            run(scores, step + 1)
            run(exponentials, step - LAG_EXP)
            run(reciprocals, step - LAG_RECIPROCAL)
            run(regroup, step - LAG_REGROUP)
            run(next_head_rows, step)
            run(store, step - LAG_STORE)
            run(weigh, step)
            run(quantise, step - LAG_QUANTISE)
            run(row_maximum, step)
